import numpy as np
import ml_dtypes


def mxq(x, axis, fmt="e4m3"):
    dtype, down = {"e4m3": (ml_dtypes.float8_e4m3fn, 7), "e5m2": (ml_dtypes.float8_e5m2, 14)}[fmt]
    v = np.moveaxis(np.asarray(x, np.float32).astype(ml_dtypes.bfloat16).astype(np.float64), axis, -1)
    blocks = v.reshape(v.shape[:-1] + (-1, 32))
    amax = np.abs(blocks).max(-1, keepdims=True)
    byte = np.maximum(np.where(amax > 0, np.frexp(amax)[1] - 1 + 127, 0) - down, 1)
    scale = np.exp2(byte - 127.0)
    codes = (blocks / scale).astype(np.float32).astype(dtype).astype(np.float64)
    return np.moveaxis((codes * scale).reshape(v.shape), -1, axis)


WIDE = False


def mx_kscale(k):
    if not WIDE:
        return np.ones(k)
    levels = np.array([10, -10, 5, -5, 0])
    a = np.random.permutation(np.resize(levels, k // 512 * 4)).reshape(k // 512, 4)
    idx = np.arange(k)
    return np.exp2(a[idx // 512, idx % 128 // 32])


BF16 = ml_dtypes.bfloat16


def bf(x):
    return np.asarray(x, np.float32).astype(BF16)


def f64(x):
    return np.asarray(x).astype(np.float64)


E2M1 = np.array([0.0, 0.5, 1.0, 1.5, 2.0, 3.0, 4.0, 6.0, -0.0, -0.5, -1.0, -1.5, -2.0, -3.0, -4.0, -6.0])


def pack_weight(w, fmt):
    k, n = w.shape
    w = f64(bf(w)).reshape(k // 32, 32, n)
    amax = np.abs(w).max(1)
    if fmt == "e4m3":
        byte = np.frexp(amax)[1] - 1 + 127 - 7
    else:
        mant, ex = np.frexp(amax / 6.0)
        byte = np.where(mant > 0.5, ex, ex - 1) + 127
    byte = np.clip(np.where(amax > 0, byte, 1), 1, 254)
    scaled = (w * np.exp2(127.0 - byte)[:, None, :]).reshape(k, n).astype(np.float32)
    by_word = np.ascontiguousarray(scaled.reshape(k // 512, 128, 4, n).transpose(0, 1, 3, 2))
    if fmt == "e4m3":
        words = by_word.astype(ml_dtypes.float8_e4m3fn).view(np.uint8)
    else:
        c = by_word.astype(ml_dtypes.float4_e2m1fn).view(np.uint8) & 0xF
        words = c[..., 0::2] | (c[..., 1::2] << 4)
    return np.ascontiguousarray(words), np.ascontiguousarray(byte.astype(np.uint8).reshape(k // 512, 16, n))


def unpack_weight(words, scales, fmt):
    g, p, n, _ = words.shape
    if fmt == "e4m3":
        vals = np.ascontiguousarray(words).view(ml_dtypes.float8_e4m3fn).astype(np.float64)
    else:
        nib = np.empty((g, p, n, 4), np.uint8)
        nib[..., 0::2] = words & 0xF
        nib[..., 1::2] = words >> 4
        vals = E2M1[nib]
    vals = vals * np.repeat(np.exp2(scales.astype(np.float64) - 127.0), 8, axis=1)[..., None]
    return vals.transpose(0, 1, 3, 2).reshape(g * 512, n)


B, K, H, D = 128, 128, 512, 64
C = 0.2
HALF_LOG_2PI = 0.5 * np.log(2.0 * np.pi)


def log_softmax(v, axis):
    v = v - v.max(axis=axis, keepdims=True)
    return v - np.log(np.exp(v).sum(axis=axis, keepdims=True))


def logsumexp(v, axis):
    m = v.max(axis=axis, keepdims=True)
    return np.log(np.exp(v - m).sum(axis=axis)) + np.squeeze(m, axis)


def contract(xq, vq):
    return (xq.transpose(2, 0, 1) @ vq.transpose(2, 1, 0)).transpose(1, 2, 0)


def setup_inputs():
    s = mx_kscale(H)[None, :, None]
    r = 1.0 / np.sqrt(H)
    x = bf(np.random.standard_normal((B, H, D)) * s)
    input_var = bf(np.random.standard_normal((B, D)) * C)
    V_alpha = np.random.standard_normal((K, H, D)) * r / s
    V_alpha_words, V_alpha_scales = pack_weight(V_alpha.reshape(-1, D), "e4m3")
    V_mu = np.random.standard_normal((K, H, D)) * C * r / s
    V_mu_words, V_mu_scales = pack_weight(V_mu.reshape(-1, D), "e4m3")
    V_sigma = np.random.standard_normal((K, H, D)) * 0.5 * r / s
    V_sigma_words, V_sigma_scales = pack_weight(V_sigma.reshape(-1, D), "e4m3")
    return {
        "x": x,
        "input_var": input_var,
        "V_alpha_words": V_alpha_words,
        "V_alpha_scales": V_alpha_scales,
        "V_mu_words": V_mu_words,
        "V_mu_scales": V_mu_scales,
        "V_sigma_words": V_sigma_words,
        "V_sigma_scales": V_sigma_scales,
        "b_alpha": bf(np.random.standard_normal((K, D)) * 0.7),
        "b_mu": bf(np.random.standard_normal((K, D)) * 0.5 * C),
        "b_sigma": bf(np.log(C) + np.random.standard_normal((K, D)) * 0.3),
    }


def reference(x, input_var, V_alpha_words, V_alpha_scales, V_mu_words, V_mu_scales, V_sigma_words, V_sigma_scales, b_alpha, b_mu, b_sigma):
    xq = mxq(f64(x), 1, "e4m3")
    exp_alpha = contract(xq, unpack_weight(V_alpha_words, V_alpha_scales, "e4m3").reshape(K, H, D)) + f64(b_alpha)
    log_alpha = log_softmax(exp_alpha, 1)
    mu = contract(xq, unpack_weight(V_mu_words, V_mu_scales, "e4m3").reshape(K, H, D)) + f64(b_mu)
    log_sigma = np.clip(contract(xq, unpack_weight(V_sigma_words, V_sigma_scales, "e4m3").reshape(K, H, D)) + f64(b_sigma), -20.0, 20.0)
    sigma = np.exp(log_sigma)
    y = f64(input_var)[:, None, :]
    log_p = -0.5 * np.square((y - mu) / sigma) + log_alpha - HALF_LOG_2PI - log_sigma
    return np.sum(logsumexp(log_p, 1), axis=1)

@@ -1,0 +1,304 @@
+from contextlib import ExitStack
+import math
+
+import concourse.mybir as mybir
+from concourse.masks import make_identity
+
+F32 = mybir.dt.float32
+BF16 = mybir.dt.bfloat16
+I32 = mybir.dt.int32
+U8 = mybir.dt.uint8
+FP8X4 = mybir.dt.float8_e4m3fn_x4
+ALU = mybir.AluOpType
+FUNC = mybir.ActivationFunctionType
+AXIS = mybir.AxisListType
+
+P = 128
+B = 128
+E = 128
+H = 512
+D = 64
+PACK = 4
+DD = 4
+DG = D // DD
+EC = 32
+NCH = E // EC
+BLK = 16
+XB = 8
+EH = 16
+HALF_LOG_2PI = 0.5 * math.log(2.0 * math.pi)
+
+FLOPS = 2 * B * E * H * D * 3
+
+
+def by_bank(ap, q, dd):
+    return ap.rearrange("p (q j i) e -> p q j i e", j=4, i=DD)[:, q, :, dd, :]
+
+
+def tile_rnadeoutputlayer_e_kernel(
+    tc,
+    x,
+    input_var,
+    V_alpha_words,
+    V_alpha_scales,
+    V_mu_words,
+    V_mu_scales,
+    V_sigma_words,
+    V_sigma_scales,
+    b_alpha,
+    b_mu,
+    b_sigma,
+    out,
+):
+    nc = tc.nc
+    words_of = {"alpha": V_alpha_words, "sigma": V_sigma_words, "mu": V_mu_words}
+    scales_of = {"alpha": V_alpha_scales, "sigma": V_sigma_scales, "mu": V_mu_scales}
+    bias_of = {"alpha": b_alpha, "sigma": b_sigma, "mu": b_mu}
+    kinds = ("alpha", "sigma", "mu")
+
+    with ExitStack() as ctx:
+        keep = ctx.enter_context(tc.tile_pool(name="keep", bufs=1))
+        wraw_pool = ctx.enter_context(tc.tile_pool(name="wraw", bufs=4))
+        psum = ctx.enter_context(tc.psum_pool(name="psum", bufs=1))
+
+        y_bf = keep.tile([P, D], BF16)
+        nc.scalar.dma_start(out=y_bf[:], in_=input_var)
+        bias_sb = {}
+        for kind in kinds:
+            bias_tile = keep.tile([P, D], BF16, name="bias_%s" % kind)
+            nc.scalar.dma_start(out=bias_tile[:], in_=bias_of[kind])
+            bias_sb[kind] = bias_tile
+        y32 = keep.tile([P, D], F32)
+        nc.vector.tensor_copy(out=y32[:], in_=y_bf[:])
+        ident_bf = keep.tile([P, P], BF16)
+        make_identity(nc, ident_bf[:])
+        ident_f32 = keep.tile([P, P], F32)
+        make_identity(nc, ident_f32[:])
+
+        xq = keep.tile([P, D, B], I32, align_bytes=64)
+        xq_scales = keep.tile([P, D, B], U8, align_bytes=64)
+        planes = {}
+        table = {}
+        for kind in kinds:
+            plane_tile = keep.tile([P, NCH, DG, EC], I32, name="planes_%s" % kind, align_bytes=64)
+            planes[kind] = plane_tile
+            table_tile = keep.tile([P, D, E], BF16, name="table_%s" % kind)
+            table[kind] = table_tile
+        least = keep.tile([P, 2, NCH, D], F32)
+        sums = keep.tile([P, 2, NCH, D], F32)
+
+        with tc.tile_pool(name="xstage", bufs=1) as xstage:
+            for kind in kinds:
+                plane_raw = xstage.tile([P, E, DG], I32, tag="plane_raw", bufs=2)
+                nc.vector.memset(plane_raw[:], 0)
+                scale_words = scales_of[kind].bitcast(F32)
+                for quad in range(4):
+                    nc.gpsimd.dma_start(
+                        out=plane_raw[32 * quad : 32 * quad + 4, :, :].bitcast(F32),
+                        in_=scale_words[:, 4 * quad : 4 * quad + 4, :].rearrange("e r g -> r e g"),
+                    )
+                nc.vector.tensor_copy(
+                    out=planes[kind][:],
+                    in_=plane_raw[:].rearrange("p (c e) g -> p c g e", c=NCH),
+                )
+
+            for kind in kinds:
+                for g8 in range(D // 8):
+                    spread = psum.tile([P, 8, E], BF16, tag="spread", bufs=2)
+                    for k in range(8):
+                        d = 8 * g8 + k
+                        nc.tensor.transpose(
+                            out=spread[:, k, :],
+                            in_=bias_sb[kind][:, d : d + 1].to_broadcast([P, P]),
+                            identity=ident_bf[:],
+                        )
+                    nc.scalar.copy(out=table[kind][:, 8 * g8 : 8 * g8 + 8, :], in_=spread[:])
+
+            grouped = xstage.tile([P, D, B, PACK], BF16, align_bytes=64)
+            for i in range(B // XB):
+                xraw = xstage.tile([P, XB, PACK * D], BF16, tag="xraw", bufs=4)
+                nc.sync.dma_start(
+                    out=xraw[:],
+                    in_=x[XB * i : XB * (i + 1), :, :].rearrange("b (p t) d -> p b (t d)", t=PACK),
+                )
+                dst = grouped[:, :, XB * i : XB * (i + 1), :]
+                src = xraw[:].rearrange("p b (t d) -> p d b t", t=PACK)
+                if i % 2 == 0:
+                    nc.vector.tensor_copy(out=dst, in_=src)
+                else:
+                    nc.scalar.copy(out=dst, in_=src)
+            for g8 in range(D // 8):
+                d_cols = slice(8 * g8, 8 * g8 + 8)
+                nc.vector.quantize_mx(
+                    out=xq[:, d_cols, :].rearrange("p d b -> p (d b)").bitcast(FP8X4),
+                    scales=xq_scales[:, d_cols, :].rearrange("p d b -> p (d b)"),
+                    in_=grouped[:, d_cols, :, :].rearrange("p d b t -> p (d b t)"),
+                )
+
+        work = ctx.enter_context(tc.tile_pool(name="work", bufs=1, reuse_waits="tile"))
+
+        def load_weight_chunk(kind, c):
+            wm = work.tile([P, DG, EC, DD], I32, tag="wm", bufs=4, align_bytes=64)
+            for half in range(EC // EH):
+                e0 = EC * c + EH * half
+                wraw = wraw_pool.tile([P, EH, D], I32, tag="wraw")
+                nc.sync.dma_start(
+                    out=wraw[:],
+                    in_=words_of[kind][e0 : e0 + EH]
+                    .rearrange("e p d t -> e p (d t)")
+                    .bitcast(I32)
+                    .rearrange("e p d -> p e d"),
+                )
+                nc.vector.tensor_copy(
+                    out=wm[:, :, EH * half : EH * (half + 1), :],
+                    in_=wraw[:].rearrange("p e (g i) -> p g e i", i=DD),
+                )
+            return wm
+
+        def mx_bank(kind, wm, c, q, dd):
+            bank = psum.tile([P, 4, EC * DD], F32, tag="mx", bufs=6)
+            for j in range(4):
+                g = 4 * q + j
+                d = DD * g + dd
+                nc.tensor.matmul_mx(
+                    out=bank[:, j, :],
+                    lhsT=xq[:, d, :].bitcast(FP8X4),
+                    lhsT_scale=xq_scales[:, d, :],
+                    rhs=wm[:, g, :, :].rearrange("p e i -> p (e i)").bitcast(FP8X4),
+                    rhs_scale=planes[kind][:, c, g, :].bitcast(U8),
+                    start=True,
+                    stop=True,
+                )
+            return bank[:].rearrange("p j (e i) -> p j e i", i=DD)[:, :, :, dd]
+
+        for c in range(NCH):
+            e_cols = slice(EC * c, EC * (c + 1))
+            neg_u = work.tile([P, D, EC], F32, tag="neg_u", bufs=2)
+            inv_sigma = work.tile([P, D, EC], F32, tag="inv_sigma", bufs=2)
+
+            wm = load_weight_chunk("alpha", c)
+            for q in range(D // BLK):
+                blk = slice(BLK * q, BLK * (q + 1))
+                for dd in range(DD):
+                    product = mx_bank("alpha", wm, c, q, dd)
+                    nc.vector.scalar_tensor_tensor(
+                        out=by_bank(neg_u[:], q, dd),
+                        in0=product,
+                        scalar=-1.0,
+                        in1=by_bank(table["alpha"][:, :, e_cols], q, dd),
+                        op0=ALU.mult,
+                        op1=ALU.subtract,
+                    )
+                nc.vector.tensor_reduce(
+                    out=least[:, 0, c, blk], in_=neg_u[:, blk, :], axis=AXIS.X, op=ALU.min
+                )
+                exp_a = work.tile([P, BLK, EC], F32, tag="exp_a", bufs=2)
+                for k in range(BLK):
+                    d = BLK * q + k
+                    nc.scalar.activation(
+                        out=exp_a[:, k, :],
+                        in_=neg_u[:, d, :],
+                        func=FUNC.Exp,
+                        bias=least[:, 0, c, d : d + 1],
+                        scale=-1.0,
+                        accum_out=sums[:, 0, c, d : d + 1],
+                    )
+
+            wm = load_weight_chunk("sigma", c)
+            for q in range(D // BLK):
+                blk = slice(BLK * q, BLK * (q + 1))
+                log_sigma = work.tile([P, BLK, EC], F32, tag="log_sigma", bufs=2)
+                for dd in range(DD):
+                    product = mx_bank("sigma", wm, c, q, dd)
+                    nc.vector.tensor_tensor(
+                        out=by_bank(log_sigma[:], 0, dd),
+                        in0=product,
+                        in1=by_bank(table["sigma"][:, :, e_cols], q, dd),
+                        op=ALU.add,
+                    )
+                nc.gpsimd.tensor_scalar(
+                    out=log_sigma[:],
+                    in0=log_sigma[:],
+                    scalar1=20.0,
+                    scalar2=-20.0,
+                    op0=ALU.min,
+                    op1=ALU.max,
+                )
+                nc.scalar.activation(
+                    out=inv_sigma[:, blk, :], in_=log_sigma[:], func=FUNC.Exp, scale=-1.0
+                )
+                nc.gpsimd.tensor_tensor(
+                    out=neg_u[:, blk, :], in0=neg_u[:, blk, :], in1=log_sigma[:], op=ALU.add
+                )
+
+            wm = load_weight_chunk("mu", c)
+            for q in range(D // BLK):
+                blk = slice(BLK * q, BLK * (q + 1))
+                neg_t = work.tile([P, BLK, EC], F32, tag="neg_t", bufs=3)
+                for dd in range(DD):
+                    product = mx_bank("mu", wm, c, q, dd)
+                    for j in range(4):
+                        d = BLK * q + DD * j + dd
+                        nc.vector.scalar_tensor_tensor(
+                            out=neg_t[:, DD * j + dd, :],
+                            in0=product[:, j, :],
+                            scalar=y32[:, d : d + 1],
+                            in1=table["mu"][:, d, e_cols],
+                            op0=ALU.subtract,
+                            op1=ALU.add,
+                        )
+                nc.gpsimd.tensor_tensor(
+                    out=neg_t[:], in0=neg_t[:], in1=inv_sigma[:, blk, :], op=ALU.mult
+                )
+                nc.scalar.activation(
+                    out=neg_t[:], in_=neg_t[:], func=FUNC.Square, scale=math.sqrt(0.5)
+                )
+                nc.gpsimd.tensor_tensor(
+                    out=neg_t[:], in0=neg_t[:], in1=neg_u[:, blk, :], op=ALU.add
+                )
+                nc.vector.tensor_reduce(
+                    out=least[:, 1, c, blk], in_=neg_t[:], axis=AXIS.X, op=ALU.min
+                )
+                for k in range(BLK):
+                    d = BLK * q + k
+                    nc.scalar.activation(
+                        out=neg_t[:, k, :],
+                        in_=neg_t[:, k, :],
+                        func=FUNC.Exp,
+                        bias=least[:, 1, c, d : d + 1],
+                        scale=-1.0,
+                        accum_out=sums[:, 1, c, d : d + 1],
+                    )
+
+        least_all = work.tile([P, 2, D], F32)
+        nc.vector.tensor_reduce(
+            out=least_all[:], in_=least[:].rearrange("p a c d -> p a d c"), axis=AXIS.X, op=ALU.min
+        )
+        weight = work.tile([P, 2, NCH, D], F32)
+        nc.vector.tensor_tensor(
+            out=weight[:],
+            in0=least[:],
+            in1=least_all[:].unsqueeze(2).to_broadcast([P, 2, NCH, D]),
+            op=ALU.subtract,
+        )
+        nc.scalar.activation(out=weight[:], in_=weight[:], func=FUNC.Exp, scale=-1.0)
+        nc.vector.tensor_tensor(out=weight[:], in0=weight[:], in1=sums[:], op=ALU.mult)
+        total = work.tile([P, 2, D], F32)
+        nc.vector.tensor_reduce(
+            out=total[:], in_=weight[:].rearrange("p a c d -> p a d c"), axis=AXIS.X, op=ALU.add
+        )
+        nc.scalar.activation(out=total[:], in_=total[:], func=FUNC.Ln)
+        lse = work.tile([P, 2, D], F32)
+        nc.vector.tensor_tensor(out=lse[:], in0=total[:], in1=least_all[:], op=ALU.subtract)
+        per_d = work.tile([P, D], F32)
+        nc.vector.tensor_tensor(out=per_d[:], in0=lse[:, 1, :], in1=lse[:, 0, :], op=ALU.subtract)
+        result = work.tile([P, 1], F32)
+        nc.vector.tensor_reduce(out=result[:], in_=per_d[:], axis=AXIS.X, op=ALU.add)
+
+        as_rows = psum.tile([P, P], F32, tag="spread", bufs=2)
+        nc.tensor.transpose(
+            out=as_rows[:], in_=result[:, 0:1].to_broadcast([P, P]), identity=ident_f32[:]
+        )
+        out_row = work.tile([P, P], F32)
+        nc.vector.tensor_scalar_add(out=out_row[:], in0=as_rows[:], scalar1=-D * HALF_LOG_2PI)
+        nc.sync.dma_start(out=out.rearrange("(o b) -> o b", o=1), in_=out_row[0:1, :])

@@ -24,8 +24,10 @@ DG = D // DD
 EC = 32
 NCH = E // EC
 BLK = 16
+QB = D // BLK
+N_BLOCKS = NCH * QB
 XB = 8
-EH = 16
+EP = EC // QB
 HALF_LOG_2PI = 0.5 * math.log(2.0 * math.pi)
 
 FLOPS = 2 * B * E * H * D * 3
@@ -57,9 +59,9 @@ def tile_rnadeoutputlayer_e_kernel(
     kinds = ("alpha", "sigma", "mu")
 
     with ExitStack() as ctx:
+        ctx.enter_context(tc.manual_schedule())
         keep = ctx.enter_context(tc.tile_pool(name="keep", bufs=1))
-        wraw_pool = ctx.enter_context(tc.tile_pool(name="wraw", bufs=4))
-        psum = ctx.enter_context(tc.psum_pool(name="psum", bufs=1))
+        wraw_pool = ctx.enter_context(tc.tile_pool(name="wraw", bufs=6))
 
         y_bf = keep.tile([P, D], BF16)
         nc.scalar.dma_start(out=y_bf[:], in_=input_var)
@@ -68,8 +70,6 @@ def tile_rnadeoutputlayer_e_kernel(
             bias_tile = keep.tile([P, D], BF16, name="bias_%s" % kind)
             nc.scalar.dma_start(out=bias_tile[:], in_=bias_of[kind])
             bias_sb[kind] = bias_tile
-        y32 = keep.tile([P, D], F32)
-        nc.vector.tensor_copy(out=y32[:], in_=y_bf[:])
         ident_bf = keep.tile([P, P], BF16)
         make_identity(nc, ident_bf[:])
         ident_f32 = keep.tile([P, P], F32)
@@ -84,35 +84,23 @@ def tile_rnadeoutputlayer_e_kernel(
             planes[kind] = plane_tile
             table_tile = keep.tile([P, D, E], BF16, name="table_%s" % kind)
             table[kind] = table_tile
+        y32 = keep.tile([P, D], F32)
         least = keep.tile([P, 2, NCH, D], F32)
         sums = keep.tile([P, 2, NCH, D], F32)
 
-        with tc.tile_pool(name="xstage", bufs=1) as xstage:
+        with tc.tile_pool(name="xstage", bufs=1) as xstage, tc.psum_pool(name="psum_x", bufs=2) as psum_x:
+            plane_raw = {}
             for kind in kinds:
-                plane_raw = xstage.tile([P, E, DG], I32, tag="plane_raw", bufs=2)
-                nc.vector.memset(plane_raw[:], 0)
+                raw_tile = xstage.tile([P, E, DG], I32, name="plane_raw_%s" % kind)
+                plane_raw[kind] = raw_tile
+                nc.vector.memset(raw_tile[:], 0)
                 scale_words = scales_of[kind].bitcast(F32)
                 for quad in range(4):
                     nc.gpsimd.dma_start(
-                        out=plane_raw[32 * quad : 32 * quad + 4, :, :].bitcast(F32),
+                        out=raw_tile[32 * quad : 32 * quad + 4, :, :].bitcast(F32),
                         in_=scale_words[:, 4 * quad : 4 * quad + 4, :].rearrange("e r g -> r e g"),
                     )
-                nc.vector.tensor_copy(
-                    out=planes[kind][:],
-                    in_=plane_raw[:].rearrange("p (c e) g -> p c g e", c=NCH),
-                )
-
-            for kind in kinds:
-                for g8 in range(D // 8):
-                    spread = psum.tile([P, 8, E], BF16, tag="spread", bufs=2)
-                    for k in range(8):
-                        d = 8 * g8 + k
-                        nc.tensor.transpose(
-                            out=spread[:, k, :],
-                            in_=bias_sb[kind][:, d : d + 1].to_broadcast([P, P]),
-                            identity=ident_bf[:],
-                        )
-                    nc.scalar.copy(out=table[kind][:, 8 * g8 : 8 * g8 + 8, :], in_=spread[:])
+            nc.vector.tensor_copy(out=y32[:], in_=y_bf[:])
 
             grouped = xstage.tile([P, D, B, PACK], BF16, align_bytes=64)
             for i in range(B // XB):
@@ -123,10 +111,28 @@ def tile_rnadeoutputlayer_e_kernel(
                 )
                 dst = grouped[:, :, XB * i : XB * (i + 1), :]
                 src = xraw[:].rearrange("p b (t d) -> p d b t", t=PACK)
-                if i % 2 == 0:
-                    nc.vector.tensor_copy(out=dst, in_=src)
-                else:
+                if i % 3 == 2:
                     nc.scalar.copy(out=dst, in_=src)
+                else:
+                    nc.vector.tensor_copy(out=dst, in_=src)
+                d_cols = slice(DD * i, DD * (i + 1))
+                for kind in kinds:
+                    spread = psum_x.tile([P, DD, E], BF16, tag="spread")
+                    for k in range(DD):
+                        d = DD * i + k
+                        nc.tensor.transpose(
+                            out=spread[:, k, :],
+                            in_=bias_sb[kind][:, d : d + 1].to_broadcast([P, P]),
+                            identity=ident_bf[:],
+                        )
+                    nc.scalar.copy(out=table[kind][:, d_cols, :], in_=spread[:])
+
+            for kind in kinds:
+                nc.vector.tensor_copy(
+                    out=planes[kind][:],
+                    in_=plane_raw[kind][:].rearrange("p (c e) g -> p c g e", c=NCH),
+                )
+
             for g8 in range(D // 8):
                 d_cols = slice(8 * g8, 8 * g8 + 8)
                 nc.vector.quantize_mx(
@@ -136,27 +142,31 @@ def tile_rnadeoutputlayer_e_kernel(
                 )
 
         work = ctx.enter_context(tc.tile_pool(name="work", bufs=1, reuse_waits="tile"))
+        psum = ctx.enter_context(tc.psum_pool(name="psum", bufs=8, reuse_waits="tile"))
 
-        def load_weight_chunk(kind, c):
-            wm = work.tile([P, DG, EC, DD], I32, tag="wm", bufs=4, align_bytes=64)
-            for half in range(EC // EH):
-                e0 = EC * c + EH * half
-                wraw = wraw_pool.tile([P, EH, D], I32, tag="wraw")
+        wm = {}
+
+        def load_part(c, part):
+            for kind in kinds:
+                if part == 0:
+                    wm_tile = work.tile([P, DG, EC, DD], I32, tag="wm", bufs=6, align_bytes=64)
+                    wm[(kind, c)] = wm_tile
+                e0 = EC * c + EP * part
+                wraw = wraw_pool.tile([P, EP, D], I32, tag="wraw")
                 nc.sync.dma_start(
                     out=wraw[:],
-                    in_=words_of[kind][e0 : e0 + EH]
+                    in_=words_of[kind][e0 : e0 + EP]
                     .rearrange("e p d t -> e p (d t)")
                     .bitcast(I32)
                     .rearrange("e p d -> p e d"),
                 )
                 nc.vector.tensor_copy(
-                    out=wm[:, :, EH * half : EH * (half + 1), :],
+                    out=wm[(kind, c)][:, :, EP * part : EP * (part + 1), :],
                     in_=wraw[:].rearrange("p e (g i) -> p g e i", i=DD),
                 )
-            return wm
 
-        def mx_bank(kind, wm, c, q, dd):
-            bank = psum.tile([P, 4, EC * DD], F32, tag="mx", bufs=6)
+        def mx_bank(kind, c, q, dd):
+            bank = psum.tile([P, 4, EC * DD], F32, tag="mx")
             for j in range(4):
                 g = 4 * q + j
                 d = DD * g + dd
@@ -164,111 +174,137 @@ def tile_rnadeoutputlayer_e_kernel(
                     out=bank[:, j, :],
                     lhsT=xq[:, d, :].bitcast(FP8X4),
                     lhsT_scale=xq_scales[:, d, :],
-                    rhs=wm[:, g, :, :].rearrange("p e i -> p (e i)").bitcast(FP8X4),
+                    rhs=wm[(kind, c)][:, g, :, :].rearrange("p e i -> p (e i)").bitcast(FP8X4),
                     rhs_scale=planes[kind][:, c, g, :].bitcast(U8),
                     start=True,
                     stop=True,
                 )
             return bank[:].rearrange("p j (e i) -> p j e i", i=DD)[:, :, :, dd]
 
-        for c in range(NCH):
+        neg_a = {}
+        log_sigma = {}
+        inv_sigma = {}
+        neg_t = {}
+
+        def products(n):
+            c, q = divmod(n, QB)
             e_cols = slice(EC * c, EC * (c + 1))
-            neg_u = work.tile([P, D, EC], F32, tag="neg_u", bufs=2)
-            inv_sigma = work.tile([P, D, EC], F32, tag="inv_sigma", bufs=2)
-
-            wm = load_weight_chunk("alpha", c)
-            for q in range(D // BLK):
-                blk = slice(BLK * q, BLK * (q + 1))
-                for dd in range(DD):
-                    product = mx_bank("alpha", wm, c, q, dd)
+            na = work.tile([P, BLK, EC], F32, tag="neg_a", bufs=5)
+            ls = work.tile([P, BLK, EC], F32, tag="log_sigma", bufs=7)
+            nt = work.tile([P, BLK, EC], F32, tag="neg_t", bufs=9)
+            neg_a[n] = na
+            log_sigma[n] = ls
+            neg_t[n] = nt
+            for dd in range(DD):
+                product = mx_bank("alpha", c, q, dd)
+                nc.vector.scalar_tensor_tensor(
+                    out=by_bank(na[:], 0, dd),
+                    in0=product,
+                    scalar=-1.0,
+                    in1=by_bank(table["alpha"][:, :, e_cols], q, dd),
+                    op0=ALU.mult,
+                    op1=ALU.subtract,
+                )
+            for dd in range(DD):
+                product = mx_bank("sigma", c, q, dd)
+                nc.vector.tensor_tensor(
+                    out=by_bank(ls[:], 0, dd),
+                    in0=product,
+                    in1=by_bank(table["sigma"][:, :, e_cols], q, dd),
+                    op=ALU.add,
+                )
+            for dd in range(DD):
+                product = mx_bank("mu", c, q, dd)
+                for j in range(4):
+                    d = BLK * q + DD * j + dd
                     nc.vector.scalar_tensor_tensor(
-                        out=by_bank(neg_u[:], q, dd),
-                        in0=product,
-                        scalar=-1.0,
-                        in1=by_bank(table["alpha"][:, :, e_cols], q, dd),
-                        op0=ALU.mult,
-                        op1=ALU.subtract,
-                    )
-                nc.vector.tensor_reduce(
-                    out=least[:, 0, c, blk], in_=neg_u[:, blk, :], axis=AXIS.X, op=ALU.min
-                )
-                exp_a = work.tile([P, BLK, EC], F32, tag="exp_a", bufs=2)
-                for k in range(BLK):
-                    d = BLK * q + k
-                    nc.scalar.activation(
-                        out=exp_a[:, k, :],
-                        in_=neg_u[:, d, :],
-                        func=FUNC.Exp,
-                        bias=least[:, 0, c, d : d + 1],
-                        scale=-1.0,
-                        accum_out=sums[:, 0, c, d : d + 1],
+                        out=nt[:, DD * j + dd, :],
+                        in0=product[:, j, :],
+                        scalar=y32[:, d : d + 1],
+                        in1=table["mu"][:, d, e_cols],
+                        op0=ALU.subtract,
+                        op1=ALU.add,
                     )
 
-            wm = load_weight_chunk("sigma", c)
-            for q in range(D // BLK):
-                blk = slice(BLK * q, BLK * (q + 1))
-                log_sigma = work.tile([P, BLK, EC], F32, tag="log_sigma", bufs=2)
-                for dd in range(DD):
-                    product = mx_bank("sigma", wm, c, q, dd)
-                    nc.vector.tensor_tensor(
-                        out=by_bank(log_sigma[:], 0, dd),
-                        in0=product,
-                        in1=by_bank(table["sigma"][:, :, e_cols], q, dd),
-                        op=ALU.add,
-                    )
-                nc.gpsimd.tensor_scalar(
-                    out=log_sigma[:],
-                    in0=log_sigma[:],
-                    scalar1=20.0,
-                    scalar2=-20.0,
-                    op0=ALU.min,
-                    op1=ALU.max,
-                )
+        def least_alpha_and_clip(n):
+            c, q = divmod(n, QB)
+            nc.vector.tensor_reduce(
+                out=least[:, 0, c, BLK * q : BLK * (q + 1)], in_=neg_a[n][:], axis=AXIS.X, op=ALU.min
+            )
+            nc.gpsimd.tensor_scalar(
+                out=log_sigma[n][:],
+                in0=log_sigma[n][:],
+                scalar1=20.0,
+                scalar2=-20.0,
+                op0=ALU.min,
+                op1=ALU.max,
+            )
+
+        def exponentials(n, which, values, results):
+            c, q = divmod(n, QB)
+            for k in range(BLK):
+                d = BLK * q + k
                 nc.scalar.activation(
-                    out=inv_sigma[:, blk, :], in_=log_sigma[:], func=FUNC.Exp, scale=-1.0
-                )
-                nc.gpsimd.tensor_tensor(
-                    out=neg_u[:, blk, :], in0=neg_u[:, blk, :], in1=log_sigma[:], op=ALU.add
+                    out=results[:, k, :],
+                    in_=values[:, k, :],
+                    func=FUNC.Exp,
+                    bias=least[:, which, c, d : d + 1],
+                    scale=-1.0,
+                    accum_out=sums[:, which, c, d : d + 1],
                 )
 
-            wm = load_weight_chunk("mu", c)
-            for q in range(D // BLK):
-                blk = slice(BLK * q, BLK * (q + 1))
-                neg_t = work.tile([P, BLK, EC], F32, tag="neg_t", bufs=3)
-                for dd in range(DD):
-                    product = mx_bank("mu", wm, c, q, dd)
-                    for j in range(4):
-                        d = BLK * q + DD * j + dd
-                        nc.vector.scalar_tensor_tensor(
-                            out=neg_t[:, DD * j + dd, :],
-                            in0=product[:, j, :],
-                            scalar=y32[:, d : d + 1],
-                            in1=table["mu"][:, d, e_cols],
-                            op0=ALU.subtract,
-                            op1=ALU.add,
-                        )
-                nc.gpsimd.tensor_tensor(
-                    out=neg_t[:], in0=neg_t[:], in1=inv_sigma[:, blk, :], op=ALU.mult
-                )
-                nc.scalar.activation(
-                    out=neg_t[:], in_=neg_t[:], func=FUNC.Square, scale=math.sqrt(0.5)
-                )
-                nc.gpsimd.tensor_tensor(
-                    out=neg_t[:], in0=neg_t[:], in1=neg_u[:, blk, :], op=ALU.add
-                )
-                nc.vector.tensor_reduce(
-                    out=least[:, 1, c, blk], in_=neg_t[:], axis=AXIS.X, op=ALU.min
-                )
-                for k in range(BLK):
-                    d = BLK * q + k
-                    nc.scalar.activation(
-                        out=neg_t[:, k, :],
-                        in_=neg_t[:, k, :],
-                        func=FUNC.Exp,
-                        bias=least[:, 1, c, d : d + 1],
-                        scale=-1.0,
-                        accum_out=sums[:, 1, c, d : d + 1],
-                    )
+        def exp_sigma_and_alpha(n):
+            inv = work.tile([P, BLK, EC], F32, tag="inv_sigma", bufs=3)
+            inv_sigma[n] = inv
+            nc.scalar.activation(out=inv[:], in_=log_sigma[n][:], func=FUNC.Exp, scale=-1.0)
+            exp_a = work.tile([P, BLK, EC], F32, tag="exp_a", bufs=2)
+            exponentials(n, 0, neg_a[n], exp_a)
+
+        def scale_and_join(n):
+            nc.gpsimd.tensor_tensor(out=neg_t[n][:], in0=neg_t[n][:], in1=inv_sigma[n][:], op=ALU.mult)
+            nc.gpsimd.tensor_tensor(out=log_sigma[n][:], in0=log_sigma[n][:], in1=neg_a[n][:], op=ALU.add)
+
+        def half_square(n):
+            nc.scalar.activation(out=neg_t[n][:], in_=neg_t[n][:], func=FUNC.Square, scale=math.sqrt(0.5))
+
+        def add_up(n):
+            nc.gpsimd.tensor_tensor(out=neg_t[n][:], in0=neg_t[n][:], in1=log_sigma[n][:], op=ALU.add)
+
+        def least_density(n):
+            c, q = divmod(n, QB)
+            nc.vector.tensor_reduce(
+                out=least[:, 1, c, BLK * q : BLK * (q + 1)], in_=neg_t[n][:], axis=AXIS.X, op=ALU.min
+            )
+
+        def exp_density(n):
+            exponentials(n, 1, neg_t[n], neg_t[n])
+
+        def live(n):
+            return 0 <= n < N_BLOCKS
+
+        for part in range(QB):
+            load_part(0, part)
+
+        for r in range(N_BLOCKS + 7):
+            if live(r - 7):
+                exp_density(r - 7)
+            if live(r - 6):
+                least_density(r - 6)
+            if live(r - 5):
+                add_up(r - 5)
+            if live(r - 4):
+                half_square(r - 4)
+            if live(r - 3):
+                scale_and_join(r - 3)
+            if live(r - 2):
+                exp_sigma_and_alpha(r - 2)
+            if live(r - 1):
+                least_alpha_and_clip(r - 1)
+            if live(r):
+                c, q = divmod(r, QB)
+                if c + 1 < NCH:
+                    load_part(c + 1, q)
+                products(r)
 
         least_all = work.tile([P, 2, D], F32)
         nc.vector.tensor_reduce(
@@ -295,7 +331,7 @@ def tile_rnadeoutputlayer_e_kernel(
         result = work.tile([P, 1], F32)
         nc.vector.tensor_reduce(out=result[:], in_=per_d[:], axis=AXIS.X, op=ALU.add)
 
-        as_rows = psum.tile([P, P], F32, tag="spread", bufs=2)
+        as_rows = psum.tile([P, P], F32, tag="mx")
         nc.tensor.transpose(
             out=as_rows[:], in_=result[:, 0:1].to_broadcast([P, P]), identity=ident_f32[:]
         )

@@ -77,11 +77,10 @@ def tile_rnadeoutputlayer_e_kernel(
 
         xq = keep.tile([P, D, B], I32, align_bytes=64)
         xq_scales = keep.tile([P, D, B], U8, align_bytes=64)
-        planes = {}
+        plane_raw = keep.tile([P, 2, len(kinds), EC, DG], I32)
+        planes = keep.tile([P, 2, len(kinds), DG, EC], I32, align_bytes=64)
         table = {}
         for kind in kinds:
-            plane_tile = keep.tile([P, NCH, DG, EC], I32, name="planes_%s" % kind, align_bytes=64)
-            planes[kind] = plane_tile
             table_tile = keep.tile([P, D, E], BF16, name="table_%s" % kind)
             table[kind] = table_tile
         y32 = keep.tile([P, D], F32)
@@ -89,17 +88,7 @@ def tile_rnadeoutputlayer_e_kernel(
         sums = keep.tile([P, 2, NCH, D], F32)
 
         with tc.tile_pool(name="xstage", bufs=1) as xstage, tc.psum_pool(name="psum_x", bufs=2) as psum_x:
-            plane_raw = {}
-            for kind in kinds:
-                raw_tile = xstage.tile([P, E, DG], I32, name="plane_raw_%s" % kind)
-                plane_raw[kind] = raw_tile
-                nc.vector.memset(raw_tile[:], 0)
-                scale_words = scales_of[kind].bitcast(F32)
-                for quad in range(4):
-                    nc.gpsimd.dma_start(
-                        out=raw_tile[32 * quad : 32 * quad + 4, :, :].bitcast(F32),
-                        in_=scale_words[:, 4 * quad : 4 * quad + 4, :].rearrange("e r g -> r e g"),
-                    )
+            nc.vector.memset(plane_raw[:], 0)
             nc.vector.tensor_copy(out=y32[:], in_=y_bf[:])
 
             grouped = xstage.tile([P, D, B, PACK], BF16, align_bytes=64)
@@ -127,12 +116,6 @@ def tile_rnadeoutputlayer_e_kernel(
                         )
                     nc.scalar.copy(out=table[kind][:, d_cols, :], in_=spread[:])
 
-            for kind in kinds:
-                nc.vector.tensor_copy(
-                    out=planes[kind][:],
-                    in_=plane_raw[kind][:].rearrange("p (c e) g -> p c g e", c=NCH),
-                )
-
             for g8 in range(D // 8):
                 d_cols = slice(8 * g8, 8 * g8 + 8)
                 nc.vector.quantize_mx(
@@ -143,6 +126,23 @@ def tile_rnadeoutputlayer_e_kernel(
 
         work = ctx.enter_context(tc.tile_pool(name="work", bufs=1, reuse_waits="tile"))
         psum = ctx.enter_context(tc.psum_pool(name="psum", bufs=8, reuse_waits="tile"))
+
+        def load_scales(c):
+            for ki, kind in enumerate(kinds):
+                scale_words = scales_of[kind].bitcast(I32)
+                for quad in range(4):
+                    nc.sync.dma_start(
+                        out=plane_raw[32 * quad : 32 * quad + 4, c % 2, ki, :, :],
+                        in_=scale_words[EC * c : EC * (c + 1), 4 * quad : 4 * quad + 4, :].rearrange(
+                            "e r g -> r e g"
+                        ),
+                    )
+
+        def regroup_scales(c):
+            nc.vector.tensor_copy(
+                out=planes[:, c % 2, :, :, :],
+                in_=plane_raw[:, c % 2, :, :, :].rearrange("p k e g -> p k g e"),
+            )
 
         wm = {}
 
@@ -175,7 +175,7 @@ def tile_rnadeoutputlayer_e_kernel(
                     lhsT=xq[:, d, :].bitcast(FP8X4),
                     lhsT_scale=xq_scales[:, d, :],
                     rhs=wm[(kind, c)][:, g, :, :].rearrange("p e i -> p (e i)").bitcast(FP8X4),
-                    rhs_scale=planes[kind][:, c, g, :].bitcast(U8),
+                    rhs_scale=planes[:, c % 2, kinds.index(kind), g, :].bitcast(U8),
                     start=True,
                     stop=True,
                 )
@@ -282,6 +282,8 @@ def tile_rnadeoutputlayer_e_kernel(
         def live(n):
             return 0 <= n < N_BLOCKS
 
+        load_scales(0)
+        regroup_scales(0)
         for part in range(QB):
             load_part(0, part)
 
@@ -303,7 +305,11 @@ def tile_rnadeoutputlayer_e_kernel(
             if live(r):
                 c, q = divmod(r, QB)
                 if c + 1 < NCH:
+                    if q == 0:
+                        load_scales(c + 1)
                     load_part(c + 1, q)
+                    if q == QB - 1:
+                        regroup_scales(c + 1)
                 products(r)
 
         least_all = work.tile([P, 2, D], F32)

@@ -13,28 +13,23 @@ ALU = mybir.AluOpType
 FUNC = mybir.ActivationFunctionType
 AXIS = mybir.AxisListType
 
+MANUAL = False
+
 P = 128
 B = 128
 E = 128
 H = 512
 D = 64
 PACK = 4
-DD = 4
-DG = D // DD
-EC = 32
-NCH = E // EC
-BLK = 16
-QB = D // BLK
-N_BLOCKS = NCH * QB
+DB = 4
+NB = D // DB
 XB = 8
-EP = EC // QB
+EP = 16
+NP = E // EP
+WRAW_BUFS = 4
 HALF_LOG_2PI = 0.5 * math.log(2.0 * math.pi)
 
 FLOPS = 2 * B * E * H * D * 3
-
-
-def by_bank(ap, q, dd):
-    return ap.rearrange("p (q j i) e -> p q j i e", j=4, i=DD)[:, q, :, dd, :]
 
 
 def tile_rnadeoutputlayer_e_kernel(
@@ -59,9 +54,11 @@ def tile_rnadeoutputlayer_e_kernel(
     kinds = ("alpha", "sigma", "mu")
 
     with ExitStack() as ctx:
-        ctx.enter_context(tc.manual_schedule())
+        if MANUAL:
+            ctx.enter_context(tc.manual_schedule())
         keep = ctx.enter_context(tc.tile_pool(name="keep", bufs=1))
-        wraw_pool = ctx.enter_context(tc.tile_pool(name="wraw", bufs=6))
+        wraw_pool = ctx.enter_context(tc.tile_pool(name="wraw", bufs=WRAW_BUFS))
+        wm_first = ctx.enter_context(tc.tile_pool(name="wm_first", bufs=1))
 
         y_bf = keep.tile([P, D], BF16)
         nc.scalar.dma_start(out=y_bf[:], in_=input_var)
@@ -77,44 +74,109 @@ def tile_rnadeoutputlayer_e_kernel(
 
         xq = keep.tile([P, D, B], I32, align_bytes=64)
         xq_scales = keep.tile([P, D, B], U8, align_bytes=64)
-        plane_raw = keep.tile([P, 2, len(kinds), EC, DG], I32)
-        planes = keep.tile([P, 2, len(kinds), DG, EC], I32, align_bytes=64)
-        table = {}
-        for kind in kinds:
-            table_tile = keep.tile([P, D, E], BF16, name="table_%s" % kind)
-            table[kind] = table_tile
-        y32 = keep.tile([P, D], F32)
-        least = keep.tile([P, 2, NCH, D], F32)
-        sums = keep.tile([P, 2, NCH, D], F32)
+        planes = keep.tile([P, D, E], U8, align_bytes=64)
+        y_table = keep.tile([P, D, B], BF16)
+        neg_ba = keep.tile([P, D], F32)
+        neg_bs = keep.tile([P, D], F32)
+        bs32 = keep.tile([P, D], F32)
+        bm32 = keep.tile([P, D], F32)
+        hi = keep.tile([P, D], F32)
+        lo = keep.tile([P, D], F32)
+        least = keep.tile([P, 2, D], F32)
+        sums = keep.tile([P, 2, D], F32)
+
+        wm = {}
+        pieces = [(kind, j) for kind in kinds for j in range(NP)]
+        wraw = {}
+
+        def load_piece(index):
+            kind, j = pieces[index]
+            raw = wraw_pool.tile([P, EP, D], I32, tag="wraw")
+            wraw[index] = raw
+            nc.sync.dma_start(
+                out=raw[:],
+                in_=words_of[kind][EP * j : EP * (j + 1)]
+                .rearrange("e p d t -> e p (d t)")
+                .bitcast(I32)
+                .rearrange("e p d -> p e d"),
+            )
+
+        def regroup_piece(index):
+            kind, j = pieces[index]
+            nc.vector.tensor_copy(
+                out=wm[kind][:, :, EP * j : EP * (j + 1)].rearrange("p (g i) e -> p g e i", i=4),
+                in_=wraw[index][:].rearrange("p e (g i) -> p g e i", i=4),
+            )
+            if index + WRAW_BUFS < len(pieces):
+                load_piece(index + WRAW_BUFS)
+
+        wm_alpha = wm_first.tile([P, D, E], I32, tag="wm", align_bytes=64)
+        wm["alpha"] = wm_alpha
 
         with tc.tile_pool(name="xstage", bufs=1) as xstage, tc.psum_pool(name="psum_x", bufs=2) as psum_x:
-            nc.vector.memset(plane_raw[:], 0)
-            nc.vector.tensor_copy(out=y32[:], in_=y_bf[:])
-
+            raw_planes = xstage.tile([P, E, D], U8)
+            nc.vector.memset(raw_planes[:].rearrange("p e d -> p (e d)").bitcast(I32), 0)
             grouped = xstage.tile([P, D, B, PACK], BF16, align_bytes=64)
-            for i in range(B // XB):
-                xraw = xstage.tile([P, XB, PACK * D], BF16, tag="xraw", bufs=4)
+            xraw = {}
+
+            def load_x(i):
+                raw = xstage.tile([P, XB, PACK * D], BF16, tag="xraw", bufs=4)
+                xraw[i] = raw
                 nc.sync.dma_start(
-                    out=xraw[:],
+                    out=raw[:],
                     in_=x[XB * i : XB * (i + 1), :, :].rearrange("b (p t) d -> p b (t d)", t=PACK),
                 )
+
+            scale_rows = [(ki, sq) for ki in range(len(kinds)) for sq in range(16)]
+
+            def load_scale_row(ki, sq):
+                row = 32 * (sq // 4) + 4 * ki + sq % 4
+                nc.sync.dma_start(
+                    out=raw_planes[row : row + 1, :, :].bitcast(I32),
+                    in_=scales_of[kinds[ki]].bitcast(I32)[:, sq : sq + 1, :].rearrange("e o g -> o e g"),
+                )
+
+            def regroup_planes(a):
+                cols = slice(16 * a, 16 * (a + 1))
+                nc.vector.tensor_copy(
+                    out=planes[:, cols, :].rearrange("p (g i) e -> p g e i", i=4),
+                    in_=raw_planes[:, :, cols].rearrange("p e (g i) -> p g e i", i=4),
+                )
+
+            for i in range(4):
+                load_x(i)
+            for i in range(B // XB):
                 dst = grouped[:, :, XB * i : XB * (i + 1), :]
-                src = xraw[:].rearrange("p b (t d) -> p d b t", t=PACK)
-                if i % 3 == 2:
+                src = xraw[i][:].rearrange("p b (t d) -> p d b t", t=PACK)
+                if i % 3 == 1:
                     nc.scalar.copy(out=dst, in_=src)
                 else:
                     nc.vector.tensor_copy(out=dst, in_=src)
-                d_cols = slice(DD * i, DD * (i + 1))
-                for kind in kinds:
-                    spread = psum_x.tile([P, DD, E], BF16, tag="spread")
-                    for k in range(DD):
-                        d = DD * i + k
-                        nc.tensor.transpose(
-                            out=spread[:, k, :],
-                            in_=bias_sb[kind][:, d : d + 1].to_broadcast([P, P]),
-                            identity=ident_bf[:],
-                        )
-                    nc.scalar.copy(out=table[kind][:, d_cols, :], in_=spread[:])
+                for ki, sq in scale_rows[6 * i : 6 * (i + 1)]:
+                    load_scale_row(ki, sq)
+                if i + 4 < B // XB:
+                    load_x(i + 4)
+                if i == 2:
+                    nc.vector.tensor_scalar(out=neg_ba[:], in0=bias_sb["alpha"][:], scalar1=-1.0, scalar2=0.0, op0=ALU.mult, op1=ALU.add)
+                    nc.vector.tensor_scalar(out=neg_bs[:], in0=bias_sb["sigma"][:], scalar1=-1.0, scalar2=0.0, op0=ALU.mult, op1=ALU.add)
+                    nc.vector.tensor_scalar(out=hi[:], in0=bias_sb["sigma"][:], scalar1=-1.0, scalar2=20.0, op0=ALU.mult, op1=ALU.add)
+                    nc.vector.tensor_scalar(out=lo[:], in0=bias_sb["sigma"][:], scalar1=-1.0, scalar2=-20.0, op0=ALU.mult, op1=ALU.add)
+                    nc.vector.tensor_copy(out=bs32[:], in_=bias_sb["sigma"][:])
+                    nc.vector.tensor_copy(out=bm32[:], in_=bias_sb["mu"][:])
+                if i >= 12:
+                    regroup_planes(i - 12)
+                spread = psum_x.tile([P, DB, B], BF16, tag="spread")
+                for k in range(DB):
+                    d = DB * i + k
+                    nc.tensor.transpose(
+                        out=spread[:, k, :],
+                        in_=y_bf[:, d : d + 1].to_broadcast([P, P]),
+                        identity=ident_bf[:],
+                    )
+                nc.scalar.copy(out=y_table[:, DB * i : DB * (i + 1), :], in_=spread[:])
+
+            for index in range(WRAW_BUFS):
+                load_piece(index)
 
             for g8 in range(D // 8):
                 d_cols = slice(8 * g8, 8 * g8 + 8)
@@ -123,224 +185,191 @@ def tile_rnadeoutputlayer_e_kernel(
                     scales=xq_scales[:, d_cols, :].rearrange("p d b -> p (d b)"),
                     in_=grouped[:, d_cols, :, :].rearrange("p d b t -> p (d b t)"),
                 )
+                if g8 % 2 == 1:
+                    regroup_piece(g8 // 2)
+            for index in range(4, NP):
+                regroup_piece(index)
 
-        work = ctx.enter_context(tc.tile_pool(name="work", bufs=1, reuse_waits="tile"))
-        psum = ctx.enter_context(tc.psum_pool(name="psum", bufs=8, reuse_waits="tile"))
+        late = ctx.enter_context(tc.tile_pool(name="late", bufs=1, reuse_waits="tile"))
+        psum_mx = ctx.enter_context(tc.psum_pool(name="psum_mx", bufs=3, reuse_waits="tile"))
+        psum_tr = ctx.enter_context(tc.psum_pool(name="psum_tr", bufs=5, reuse_waits="tile"))
 
-        def load_scales(c):
-            for ki, kind in enumerate(kinds):
-                scale_words = scales_of[kind].bitcast(I32)
-                for quad in range(4):
-                    nc.sync.dma_start(
-                        out=plane_raw[32 * quad : 32 * quad + 4, c % 2, ki, :, :],
-                        in_=scale_words[EC * c : EC * (c + 1), 4 * quad : 4 * quad + 4, :].rearrange(
-                            "e r g -> r e g"
-                        ),
-                    )
+        neg_a = late.tile([P, D, B], F32)
+        inv_sigma = late.tile([P, D, B], F32)
+        wm_sigma = late.tile([P, D, E], I32, align_bytes=64)
+        wm["sigma"] = wm_sigma
 
-        def regroup_scales(c):
-            nc.vector.tensor_copy(
-                out=planes[:, c % 2, :, :, :],
-                in_=plane_raw[:, c % 2, :, :, :].rearrange("p k e g -> p k g e"),
-            )
+        banks = {}
+        turned = {}
+        clipped = {}
+        dev = {}
 
-        wm = {}
-
-        def load_part(c, part):
-            for kind in kinds:
-                if part == 0:
-                    wm_tile = work.tile([P, DG, EC, DD], I32, tag="wm", bufs=6, align_bytes=64)
-                    wm[(kind, c)] = wm_tile
-                e0 = EC * c + EP * part
-                wraw = wraw_pool.tile([P, EP, D], I32, tag="wraw")
-                nc.sync.dma_start(
-                    out=wraw[:],
-                    in_=words_of[kind][e0 : e0 + EP]
-                    .rearrange("e p d t -> e p (d t)")
-                    .bitcast(I32)
-                    .rearrange("e p d -> p e d"),
-                )
-                nc.vector.tensor_copy(
-                    out=wm[(kind, c)][:, :, EP * part : EP * (part + 1), :],
-                    in_=wraw[:].rearrange("p e (g i) -> p g e i", i=DD),
-                )
-
-        def mx_bank(kind, c, q, dd):
-            bank = psum.tile([P, 4, EC * DD], F32, tag="mx")
-            for j in range(4):
-                g = 4 * q + j
-                d = DD * g + dd
+        def products(kind, n):
+            bank = psum_mx.tile([P, DB, B], F32, tag="mx")
+            banks[(kind, n)] = bank
+            first_row = 4 * kinds.index(kind)
+            for k in range(DB):
+                d = DB * n + k
                 nc.tensor.matmul_mx(
-                    out=bank[:, j, :],
-                    lhsT=xq[:, d, :].bitcast(FP8X4),
-                    lhsT_scale=xq_scales[:, d, :],
-                    rhs=wm[(kind, c)][:, g, :, :].rearrange("p e i -> p (e i)").bitcast(FP8X4),
-                    rhs_scale=planes[:, c % 2, kinds.index(kind), g, :].bitcast(U8),
+                    out=bank[:, k, :],
+                    lhsT=wm[kind][:, d, :].bitcast(FP8X4),
+                    lhsT_scale=planes[first_row:P, d, :],
+                    rhs=xq[:, d, :].bitcast(FP8X4),
+                    rhs_scale=xq_scales[:, d, :],
                     start=True,
                     stop=True,
                 )
-            return bank[:].rearrange("p j (e i) -> p j e i", i=DD)[:, :, :, dd]
 
-        neg_a = {}
-        log_sigma = {}
-        inv_sigma = {}
-        neg_t = {}
-
-        def products(n):
-            c, q = divmod(n, QB)
-            e_cols = slice(EC * c, EC * (c + 1))
-            na = work.tile([P, BLK, EC], F32, tag="neg_a", bufs=5)
-            ls = work.tile([P, BLK, EC], F32, tag="log_sigma", bufs=7)
-            nt = work.tile([P, BLK, EC], F32, tag="neg_t", bufs=9)
-            neg_a[n] = na
-            log_sigma[n] = ls
-            neg_t[n] = nt
-            for dd in range(DD):
-                product = mx_bank("alpha", c, q, dd)
-                nc.vector.scalar_tensor_tensor(
-                    out=by_bank(na[:], 0, dd),
-                    in0=product,
-                    scalar=-1.0,
-                    in1=by_bank(table["alpha"][:, :, e_cols], q, dd),
-                    op0=ALU.mult,
-                    op1=ALU.subtract,
-                )
-            for dd in range(DD):
-                product = mx_bank("sigma", c, q, dd)
-                nc.vector.tensor_tensor(
-                    out=by_bank(ls[:], 0, dd),
-                    in0=product,
-                    in1=by_bank(table["sigma"][:, :, e_cols], q, dd),
-                    op=ALU.add,
-                )
-            for dd in range(DD):
-                product = mx_bank("mu", c, q, dd)
-                for j in range(4):
-                    d = BLK * q + DD * j + dd
-                    nc.vector.scalar_tensor_tensor(
-                        out=nt[:, DD * j + dd, :],
-                        in0=product[:, j, :],
-                        scalar=y32[:, d : d + 1],
-                        in1=table["mu"][:, d, e_cols],
-                        op0=ALU.subtract,
-                        op1=ALU.add,
-                    )
-
-        def least_alpha_and_clip(n):
-            c, q = divmod(n, QB)
-            nc.vector.tensor_reduce(
-                out=least[:, 0, c, BLK * q : BLK * (q + 1)], in_=neg_a[n][:], axis=AXIS.X, op=ALU.min
-            )
-            nc.gpsimd.tensor_scalar(
-                out=log_sigma[n][:],
-                in0=log_sigma[n][:],
-                scalar1=20.0,
-                scalar2=-20.0,
-                op0=ALU.min,
-                op1=ALU.max,
-            )
-
-        def exponentials(n, which, values, results):
-            c, q = divmod(n, QB)
-            for k in range(BLK):
-                d = BLK * q + k
+        def take_alpha(n):
+            for k in range(DB):
+                d = DB * n + k
                 nc.scalar.activation(
-                    out=results[:, k, :],
-                    in_=values[:, k, :],
-                    func=FUNC.Exp,
-                    bias=least[:, which, c, d : d + 1],
-                    scale=-1.0,
-                    accum_out=sums[:, which, c, d : d + 1],
+                    out=neg_a[:, d, :], in_=banks[("alpha", n)][:, k, :], func=FUNC.Identity,
+                    bias=neg_ba[:, d : d + 1], scale=-1.0,
                 )
 
-        def exp_sigma_and_alpha(n):
-            inv = work.tile([P, BLK, EC], F32, tag="inv_sigma", bufs=3)
-            inv_sigma[n] = inv
-            nc.scalar.activation(out=inv[:], in_=log_sigma[n][:], func=FUNC.Exp, scale=-1.0)
-            exp_a = work.tile([P, BLK, EC], F32, tag="exp_a", bufs=2)
-            exponentials(n, 0, neg_a[n], exp_a)
+        def turn_alpha(n):
+            bank = psum_tr.tile([P, DB, E], F32, tag="tr")
+            turned[(0, n)] = bank
+            for k in range(DB):
+                nc.tensor.transpose(out=bank[:, k, :], in_=neg_a[:, DB * n + k, :], identity=ident_f32[:])
 
-        def scale_and_join(n):
-            nc.gpsimd.tensor_tensor(out=neg_t[n][:], in0=neg_t[n][:], in1=inv_sigma[n][:], op=ALU.mult)
-            nc.gpsimd.tensor_tensor(out=log_sigma[n][:], in0=log_sigma[n][:], in1=neg_a[n][:], op=ALU.add)
+        def least_of(which, n):
+            nc.vector.tensor_reduce(
+                out=least[:, which, DB * n : DB * (n + 1)], in_=turned[(which, n)][:], axis=AXIS.X, op=ALU.min
+            )
+
+        def exponentials(which, n):
+            for k in range(DB):
+                d = DB * n + k
+                exp_out = late.tile([P, E], BF16, tag="exp_out", bufs=2)
+                nc.scalar.activation(
+                    out=exp_out[:], in_=turned[(which, n)][:, k, :], func=FUNC.Exp,
+                    bias=least[:, which, d : d + 1], scale=-1.0, accum_out=sums[:, which, d : d + 1],
+                )
+
+        def take_sigma(n):
+            sc = late.tile([P, DB, B], F32, tag="clipped", bufs=3)
+            clipped[n] = sc
+            for k in range(DB):
+                d = DB * n + k
+                nc.vector.tensor_scalar(
+                    out=sc[:, k, :], in0=banks[("sigma", n)][:, k, :],
+                    scalar1=hi[:, d : d + 1], scalar2=lo[:, d : d + 1], op0=ALU.min, op1=ALU.max,
+                )
+
+        def exp_sigma(n):
+            for k in range(DB):
+                d = DB * n + k
+                nc.scalar.activation(
+                    out=inv_sigma[:, d, :], in_=clipped[n][:, k, :], func=FUNC.Exp,
+                    bias=neg_bs[:, d : d + 1], scale=-1.0,
+                )
+
+        def join(n):
+            cols = slice(DB * n, DB * (n + 1))
+            nc.gpsimd.tensor_tensor(out=neg_a[:, cols, :], in0=neg_a[:, cols, :], in1=clipped[n][:], op=ALU.add)
+
+        def take_mu(n):
+            m = late.tile([P, DB, B], F32, tag="dev", bufs=5)
+            dev[n] = m
+            for k in range(DB):
+                d = DB * n + k
+                nc.vector.scalar_tensor_tensor(
+                    out=m[:, k, :], in0=banks[("mu", n)][:, k, :], scalar=bm32[:, d : d + 1],
+                    in1=y_table[:, d, :], op0=ALU.add, op1=ALU.subtract,
+                )
+
+        def scale_dev(n):
+            cols = slice(DB * n, DB * (n + 1))
+            nc.gpsimd.tensor_tensor(out=dev[n][:], in0=dev[n][:], in1=inv_sigma[:, cols, :], op=ALU.mult)
 
         def half_square(n):
-            nc.scalar.activation(out=neg_t[n][:], in_=neg_t[n][:], func=FUNC.Square, scale=math.sqrt(0.5))
+            nc.scalar.activation(out=dev[n][:], in_=dev[n][:], func=FUNC.Square, scale=math.sqrt(0.5))
 
-        def add_up(n):
-            nc.gpsimd.tensor_tensor(out=neg_t[n][:], in0=neg_t[n][:], in1=log_sigma[n][:], op=ALU.add)
+        def turn_open(n):
+            bank = psum_tr.tile([P, DB, E], F32, tag="tr")
+            turned[(1, n)] = bank
+            for k in range(DB):
+                d = DB * n + k
+                nc.tensor.matmul(
+                    out=bank[:, k, :], lhsT=bs32[:, d : d + 1].to_broadcast([P, P]), rhs=ident_f32[:],
+                    is_transpose=True, start=(k == 0), stop=False,
+                )
+            for k in range(DB):
+                nc.tensor.matmul(
+                    out=bank[:, k, :], lhsT=neg_a[:, DB * n + k, :], rhs=ident_f32[:],
+                    is_transpose=True, start=False, stop=False,
+                )
 
-        def least_density(n):
-            c, q = divmod(n, QB)
-            nc.vector.tensor_reduce(
-                out=least[:, 1, c, BLK * q : BLK * (q + 1)], in_=neg_t[n][:], axis=AXIS.X, op=ALU.min
-            )
+        def turn_close(n):
+            bank = turned[(1, n)]
+            for k in range(DB):
+                nc.tensor.matmul(
+                    out=bank[:, k, :], lhsT=dev[n][:, k, :], rhs=ident_f32[:],
+                    is_transpose=True, start=False, stop=(k == DB - 1),
+                )
 
-        def exp_density(n):
-            exponentials(n, 1, neg_t[n], neg_t[n])
+        def step(t):
+            if 0 <= t < 3 * NB:
+                return kinds[t // NB], t % NB
+            return None, 0
 
-        def live(n):
-            return 0 <= n < N_BLOCKS
+        for t in range(3 * NB + 7):
+            kind, n = step(t - 6)
+            if kind == "mu":
+                exponentials(1, n)
+            kind, n = step(t - 5)
+            if kind == "mu":
+                least_of(1, n)
+            kind, n = step(t - 4)
+            if kind == "alpha":
+                exponentials(0, n)
+            if kind == "mu":
+                turn_close(n)
+            kind, n = step(t - 3)
+            if kind == "alpha":
+                least_of(0, n)
+            if kind == "mu":
+                half_square(n)
+                turn_open(n)
+            kind, n = step(t - 2)
+            if kind == "alpha":
+                turn_alpha(n)
+            if kind == "sigma":
+                exp_sigma(n)
+                join(n)
+            if kind == "mu":
+                scale_dev(n)
+            kind, n = step(t - 1)
+            if kind == "alpha":
+                take_alpha(n)
+            if kind == "sigma":
+                take_sigma(n)
+            if kind == "mu":
+                take_mu(n)
+            if t < 2 * NB and t % 2 == 0:
+                if t == NB:
+                    wm_mu = wm_first.tile([P, D, E], I32, tag="wm", align_bytes=64)
+                    wm["mu"] = wm_mu
+                regroup_piece(NP + t // 2)
+            kind, n = step(t)
+            if kind is not None:
+                products(kind, n)
 
-        load_scales(0)
-        regroup_scales(0)
-        for part in range(QB):
-            load_part(0, part)
-
-        for r in range(N_BLOCKS + 7):
-            if live(r - 7):
-                exp_density(r - 7)
-            if live(r - 6):
-                least_density(r - 6)
-            if live(r - 5):
-                add_up(r - 5)
-            if live(r - 4):
-                half_square(r - 4)
-            if live(r - 3):
-                scale_and_join(r - 3)
-            if live(r - 2):
-                exp_sigma_and_alpha(r - 2)
-            if live(r - 1):
-                least_alpha_and_clip(r - 1)
-            if live(r):
-                c, q = divmod(r, QB)
-                if c + 1 < NCH:
-                    if q == 0:
-                        load_scales(c + 1)
-                    load_part(c + 1, q)
-                    if q == QB - 1:
-                        regroup_scales(c + 1)
-                products(r)
-
-        least_all = work.tile([P, 2, D], F32)
-        nc.vector.tensor_reduce(
-            out=least_all[:], in_=least[:].rearrange("p a c d -> p a d c"), axis=AXIS.X, op=ALU.min
-        )
-        weight = work.tile([P, 2, NCH, D], F32)
-        nc.vector.tensor_tensor(
-            out=weight[:],
-            in0=least[:],
-            in1=least_all[:].unsqueeze(2).to_broadcast([P, 2, NCH, D]),
-            op=ALU.subtract,
-        )
-        nc.scalar.activation(out=weight[:], in_=weight[:], func=FUNC.Exp, scale=-1.0)
-        nc.vector.tensor_tensor(out=weight[:], in0=weight[:], in1=sums[:], op=ALU.mult)
-        total = work.tile([P, 2, D], F32)
-        nc.vector.tensor_reduce(
-            out=total[:], in_=weight[:].rearrange("p a c d -> p a d c"), axis=AXIS.X, op=ALU.add
-        )
-        nc.scalar.activation(out=total[:], in_=total[:], func=FUNC.Ln)
-        lse = work.tile([P, 2, D], F32)
-        nc.vector.tensor_tensor(out=lse[:], in0=total[:], in1=least_all[:], op=ALU.subtract)
-        per_d = work.tile([P, D], F32)
+        total = late.tile([P, 2, D], F32)
+        nc.scalar.activation(out=total[:], in_=sums[:], func=FUNC.Ln)
+        lse = late.tile([P, 2, D], F32)
+        nc.vector.tensor_tensor(out=lse[:], in0=total[:], in1=least[:], op=ALU.subtract)
+        per_d = late.tile([P, D], F32)
         nc.vector.tensor_tensor(out=per_d[:], in0=lse[:, 1, :], in1=lse[:, 0, :], op=ALU.subtract)
-        result = work.tile([P, 1], F32)
+        result = late.tile([P, 1], F32)
         nc.vector.tensor_reduce(out=result[:], in_=per_d[:], axis=AXIS.X, op=ALU.add)
 
-        as_rows = psum.tile([P, P], F32, tag="mx")
+        as_rows = psum_tr.tile([P, P], F32, tag="tr")
         nc.tensor.transpose(
             out=as_rows[:], in_=result[:, 0:1].to_broadcast([P, P]), identity=ident_f32[:]
         )
-        out_row = work.tile([P, P], F32)
+        out_row = late.tile([P, P], F32)
         nc.vector.tensor_scalar_add(out=out_row[:], in0=as_rows[:], scalar1=-D * HALF_LOG_2PI)
         nc.sync.dma_start(out=out.rearrange("(o b) -> o b", o=1), in_=out_row[0:1, :])

@@ -13,7 +13,7 @@ ALU = mybir.AluOpType
 FUNC = mybir.ActivationFunctionType
 AXIS = mybir.AxisListType
 
-MANUAL = False
+MANUAL = True
 
 P = 128
 B = 128

@@ -91,7 +91,7 @@ def tile_rnadeoutputlayer_e_kernel(
 
         def load_piece(index):
             kind, j = pieces[index]
-            raw = wraw_pool.tile([P, EP, D], I32, tag="wraw")
+            raw = wraw_pool.tile([P, EP, D], I32, tag="wraw", align_bytes=1024)
             wraw[index] = raw
             nc.sync.dma_start(
                 out=raw[:],
@@ -114,13 +114,13 @@ def tile_rnadeoutputlayer_e_kernel(
         wm["alpha"] = wm_alpha
 
         with tc.tile_pool(name="xstage", bufs=1) as xstage, tc.psum_pool(name="psum_x", bufs=2) as psum_x:
-            raw_planes = xstage.tile([P, E, D], U8)
+            raw_planes = xstage.tile([P, E, D], U8, align_bytes=1024)
             nc.vector.memset(raw_planes[:].rearrange("p e d -> p (e d)").bitcast(I32), 0)
             grouped = xstage.tile([P, D, B, PACK], BF16, align_bytes=64)
             xraw = {}
 
             def load_x(i):
-                raw = xstage.tile([P, XB, PACK * D], BF16, tag="xraw", bufs=4)
+                raw = xstage.tile([P, XB, PACK * D], BF16, tag="xraw", bufs=4, align_bytes=1024)
                 xraw[i] = raw
                 nc.sync.dma_start(
                     out=raw[:],

@@ -127,13 +127,19 @@ def tile_rnadeoutputlayer_e_kernel(
                     in_=x[XB * i : XB * (i + 1), :, :].rearrange("b (p t) d -> p b (t d)", t=PACK),
                 )
 
-            scale_rows = [(ki, sq) for ki in range(len(kinds)) for sq in range(16)]
-
-            def load_scale_row(ki, sq):
-                row = 32 * (sq // 4) + 4 * ki + sq % 4
+            staged_planes = xstage.tile([P, E, D], U8, align_bytes=1024)
+            for ki in range(len(kinds)):
                 nc.sync.dma_start(
-                    out=raw_planes[row : row + 1, :, :].bitcast(I32),
-                    in_=scales_of[kinds[ki]].bitcast(I32)[:, sq : sq + 1, :].rearrange("e o g -> o e g"),
+                    out=staged_planes[32 * ki : 32 * ki + 16, :, :].bitcast(I32),
+                    in_=scales_of[kinds[ki]].bitcast(I32).rearrange("e q g -> q e g"),
+                )
+
+            scale_moves = [(ki, quad) for ki in range(len(kinds)) for quad in range(4)]
+
+            def move_scale_rows(ki, quad):
+                nc.sync.dma_start(
+                    out=raw_planes[32 * quad + 4 * ki : 32 * quad + 4 * ki + 4, :, :].bitcast(I32),
+                    in_=staged_planes[32 * ki + 4 * quad : 32 * ki + 4 * quad + 4, :, :].bitcast(I32),
                 )
 
             def regroup_planes(a):
@@ -152,8 +158,8 @@ def tile_rnadeoutputlayer_e_kernel(
                     nc.scalar.copy(out=dst, in_=src)
                 else:
                     nc.vector.tensor_copy(out=dst, in_=src)
-                for ki, sq in scale_rows[6 * i : 6 * (i + 1)]:
-                    load_scale_row(ki, sq)
+                for ki, quad in scale_moves[6 * i : 6 * (i + 1)]:
+                    move_scale_rows(ki, quad)
                 if i + 4 < B // XB:
                     load_x(i + 4)
                 if i == 2:

@@ -24,6 +24,7 @@ PACK = 4
 DB = 4
 NB = D // DB
 XB = 8
+XRAW_BUFS = 8
 EP = 16
 NP = E // EP
 WRAW_BUFS = 4
@@ -120,7 +121,7 @@ def tile_rnadeoutputlayer_e_kernel(
             xraw = {}
 
             def load_x(i):
-                raw = xstage.tile([P, XB, PACK * D], BF16, tag="xraw", bufs=4, align_bytes=1024)
+                raw = xstage.tile([P, XB, PACK * D], BF16, tag="xraw", bufs=XRAW_BUFS, align_bytes=1024)
                 xraw[i] = raw
                 nc.sync.dma_start(
                     out=raw[:],
@@ -149,7 +150,7 @@ def tile_rnadeoutputlayer_e_kernel(
                     in_=raw_planes[:, :, cols].rearrange("p e (g i) -> p g e i", i=4),
                 )
 
-            for i in range(4):
+            for i in range(XRAW_BUFS):
                 load_x(i)
             for i in range(B // XB):
                 dst = grouped[:, :, XB * i : XB * (i + 1), :]
@@ -160,8 +161,8 @@ def tile_rnadeoutputlayer_e_kernel(
                     nc.vector.tensor_copy(out=dst, in_=src)
                 for ki, quad in scale_moves[6 * i : 6 * (i + 1)]:
                     move_scale_rows(ki, quad)
-                if i + 4 < B // XB:
-                    load_x(i + 4)
+                if i + XRAW_BUFS < B // XB:
+                    load_x(i + XRAW_BUFS)
                 if i == 2:
                     nc.vector.tensor_scalar(out=neg_ba[:], in0=bias_sb["alpha"][:], scalar1=-1.0, scalar2=0.0, op0=ALU.mult, op1=ALU.add)
                     nc.vector.tensor_scalar(out=neg_bs[:], in0=bias_sb["sigma"][:], scalar1=-1.0, scalar2=0.0, op0=ALU.mult, op1=ALU.add)

@@ -153,8 +153,8 @@ def tile_rnadeoutputlayer_e_kernel(
             for i in range(XRAW_BUFS):
                 load_x(i)
             for i in range(B // XB):
-                dst = grouped[:, :, XB * i : XB * (i + 1), :]
-                src = xraw[i][:].rearrange("p b (t d) -> p d b t", t=PACK)
+                dst = grouped[:, :, XB * i : XB * (i + 1), :].rearrange("p (c i) b t -> p c (b t) i", i=4)
+                src = xraw[i][:].rearrange("p b (t c i) -> p c (b t) i", t=PACK, i=4)
                 if i % 3 == 1:
                     nc.scalar.copy(out=dst, in_=src)
                 else:

@@ -27,7 +27,8 @@ XB = 8
 XRAW_BUFS = 8
 EP = 16
 NP = E // EP
-WRAW_BUFS = 4
+WRAW_BUFS = 6
+AHEAD = 4
 HALF_LOG_2PI = 0.5 * math.log(2.0 * math.pi)
 
 FLOPS = 2 * B * E * H * D * 3
@@ -79,7 +80,6 @@ def tile_rnadeoutputlayer_e_kernel(
         y_table = keep.tile([P, D, B], BF16)
         neg_ba = keep.tile([P, D], F32)
         neg_bs = keep.tile([P, D], F32)
-        bs32 = keep.tile([P, D], F32)
         bm32 = keep.tile([P, D], F32)
         hi = keep.tile([P, D], F32)
         lo = keep.tile([P, D], F32)
@@ -164,11 +164,10 @@ def tile_rnadeoutputlayer_e_kernel(
                 if i + XRAW_BUFS < B // XB:
                     load_x(i + XRAW_BUFS)
                 if i == 2:
-                    nc.vector.tensor_scalar(out=neg_ba[:], in0=bias_sb["alpha"][:], scalar1=-1.0, scalar2=0.0, op0=ALU.mult, op1=ALU.add)
+                    nc.vector.tensor_tensor(out=neg_ba[:], in0=bias_sb["sigma"][:], in1=bias_sb["alpha"][:], op=ALU.subtract)
                     nc.vector.tensor_scalar(out=neg_bs[:], in0=bias_sb["sigma"][:], scalar1=-1.0, scalar2=0.0, op0=ALU.mult, op1=ALU.add)
                     nc.vector.tensor_scalar(out=hi[:], in0=bias_sb["sigma"][:], scalar1=-1.0, scalar2=20.0, op0=ALU.mult, op1=ALU.add)
                     nc.vector.tensor_scalar(out=lo[:], in0=bias_sb["sigma"][:], scalar1=-1.0, scalar2=-20.0, op0=ALU.mult, op1=ALU.add)
-                    nc.vector.tensor_copy(out=bs32[:], in_=bias_sb["sigma"][:])
                     nc.vector.tensor_copy(out=bm32[:], in_=bias_sb["mu"][:])
                 if i >= 12:
                     regroup_planes(i - 12)
@@ -198,17 +197,17 @@ def tile_rnadeoutputlayer_e_kernel(
                 regroup_piece(index)
 
         late = ctx.enter_context(tc.tile_pool(name="late", bufs=1, reuse_waits="tile"))
-        psum_mx = ctx.enter_context(tc.psum_pool(name="psum_mx", bufs=3, reuse_waits="tile"))
-        psum_tr = ctx.enter_context(tc.psum_pool(name="psum_tr", bufs=5, reuse_waits="tile"))
+        psum_mx = ctx.enter_context(tc.psum_pool(name="psum_mx", bufs=4, reuse_waits="tile"))
+        psum_tr = ctx.enter_context(tc.psum_pool(name="psum_tr", bufs=4, reuse_waits="tile"))
 
         neg_a = late.tile([P, D, B], F32)
-        inv_sigma = late.tile([P, D, B], F32)
         wm_sigma = late.tile([P, D, E], I32, align_bytes=64)
         wm["sigma"] = wm_sigma
 
         banks = {}
         turned = {}
         clipped = {}
+        inv_sigma = {}
         dev = {}
 
         def products(kind, n):
@@ -239,7 +238,16 @@ def tile_rnadeoutputlayer_e_kernel(
             bank = psum_tr.tile([P, DB, E], F32, tag="tr")
             turned[(0, n)] = bank
             for k in range(DB):
-                nc.tensor.transpose(out=bank[:, k, :], in_=neg_a[:, DB * n + k, :], identity=ident_f32[:])
+                d = DB * n + k
+                nc.tensor.matmul(
+                    out=bank[:, k, :], lhsT=neg_bs[:, d : d + 1].to_broadcast([P, P]), rhs=ident_f32[:],
+                    is_transpose=True, start=(k == 0), stop=False,
+                )
+            for k in range(DB):
+                nc.tensor.matmul(
+                    out=bank[:, k, :], lhsT=neg_a[:, DB * n + k, :], rhs=ident_f32[:],
+                    is_transpose=True, start=False, stop=(k == DB - 1),
+                )
 
         def least_of(which, n):
             nc.vector.tensor_reduce(
@@ -256,7 +264,7 @@ def tile_rnadeoutputlayer_e_kernel(
                 )
 
         def take_sigma(n):
-            sc = late.tile([P, DB, B], F32, tag="clipped", bufs=3)
+            sc = late.tile([P, DB, B], F32, tag="clipped", bufs=6 + AHEAD)
             clipped[n] = sc
             for k in range(DB):
                 d = DB * n + k
@@ -266,19 +274,17 @@ def tile_rnadeoutputlayer_e_kernel(
                 )
 
         def exp_sigma(n):
+            inv = late.tile([P, DB, B], F32, tag="inv", bufs=3 + AHEAD)
+            inv_sigma[n] = inv
             for k in range(DB):
                 d = DB * n + k
                 nc.scalar.activation(
-                    out=inv_sigma[:, d, :], in_=clipped[n][:, k, :], func=FUNC.Exp,
+                    out=inv[:, k, :], in_=clipped[n][:, k, :], func=FUNC.Exp,
                     bias=neg_bs[:, d : d + 1], scale=-1.0,
                 )
 
-        def join(n):
-            cols = slice(DB * n, DB * (n + 1))
-            nc.gpsimd.tensor_tensor(out=neg_a[:, cols, :], in0=neg_a[:, cols, :], in1=clipped[n][:], op=ALU.add)
-
         def take_mu(n):
-            m = late.tile([P, DB, B], F32, tag="dev", bufs=5)
+            m = late.tile([P, DB, B], F32, tag="dev", bufs=6)
             dev[n] = m
             for k in range(DB):
                 d = DB * n + k
@@ -288,81 +294,73 @@ def tile_rnadeoutputlayer_e_kernel(
                 )
 
         def scale_dev(n):
-            cols = slice(DB * n, DB * (n + 1))
-            nc.gpsimd.tensor_tensor(out=dev[n][:], in0=dev[n][:], in1=inv_sigma[:, cols, :], op=ALU.mult)
+            nc.gpsimd.tensor_tensor(out=dev[n][:], in0=dev[n][:], in1=inv_sigma[n][:], op=ALU.mult)
 
         def half_square(n):
             nc.scalar.activation(out=dev[n][:], in_=dev[n][:], func=FUNC.Square, scale=math.sqrt(0.5))
 
-        def turn_open(n):
+        def turn_density(n):
             bank = psum_tr.tile([P, DB, E], F32, tag="tr")
             turned[(1, n)] = bank
             for k in range(DB):
-                d = DB * n + k
                 nc.tensor.matmul(
-                    out=bank[:, k, :], lhsT=bs32[:, d : d + 1].to_broadcast([P, P]), rhs=ident_f32[:],
+                    out=bank[:, k, :], lhsT=neg_a[:, DB * n + k, :], rhs=ident_f32[:],
                     is_transpose=True, start=(k == 0), stop=False,
                 )
             for k in range(DB):
                 nc.tensor.matmul(
-                    out=bank[:, k, :], lhsT=neg_a[:, DB * n + k, :], rhs=ident_f32[:],
+                    out=bank[:, k, :], lhsT=clipped[n][:, k, :], rhs=ident_f32[:],
                     is_transpose=True, start=False, stop=False,
                 )
-
-        def turn_close(n):
-            bank = turned[(1, n)]
             for k in range(DB):
                 nc.tensor.matmul(
                     out=bank[:, k, :], lhsT=dev[n][:, k, :], rhs=ident_f32[:],
                     is_transpose=True, start=False, stop=(k == DB - 1),
                 )
 
-        def step(t):
-            if 0 <= t < 3 * NB:
-                return kinds[t // NB], t % NB
-            return None, 0
+        def within(n):
+            return 0 <= n < NB
 
-        for t in range(3 * NB + 7):
-            kind, n = step(t - 6)
-            if kind == "mu":
-                exponentials(1, n)
-            kind, n = step(t - 5)
-            if kind == "mu":
-                least_of(1, n)
-            kind, n = step(t - 4)
-            if kind == "alpha":
-                exponentials(0, n)
-            if kind == "mu":
-                turn_close(n)
-            kind, n = step(t - 3)
-            if kind == "alpha":
-                least_of(0, n)
-            if kind == "mu":
-                half_square(n)
-                turn_open(n)
-            kind, n = step(t - 2)
-            if kind == "alpha":
-                turn_alpha(n)
-            if kind == "sigma":
-                exp_sigma(n)
-                join(n)
-            if kind == "mu":
-                scale_dev(n)
-            kind, n = step(t - 1)
-            if kind == "alpha":
-                take_alpha(n)
-            if kind == "sigma":
-                take_sigma(n)
-            if kind == "mu":
-                take_mu(n)
+        for t in range(3 * NB + 8):
+            first = t
+            second = t - NB
+            third = t - 2 * NB
+            early = third + AHEAD
+            if within(third - 7):
+                exponentials(1, third - 7)
+            if within(third - 6):
+                least_of(1, third - 6)
+            if within(third - 5):
+                turn_density(third - 5)
+            if within(third - 4):
+                half_square(third - 4)
+            if within(third - 3):
+                scale_dev(third - 3)
+            if within(early - 2):
+                exp_sigma(early - 2)
+            if within(second - 2):
+                exponentials(0, second - 2)
+            if within(second - 1):
+                least_of(0, second - 1)
+            if within(early - 1):
+                take_sigma(early - 1)
+            if within(third - 1):
+                take_mu(third - 1)
+            if within(first - 1):
+                take_alpha(first - 1)
             if t < 2 * NB and t % 2 == 0:
                 if t == NB:
                     wm_mu = wm_first.tile([P, D, E], I32, tag="wm", align_bytes=64)
                     wm["mu"] = wm_mu
                 regroup_piece(NP + t // 2)
-            kind, n = step(t)
-            if kind is not None:
-                products(kind, n)
+            if within(second):
+                turn_alpha(second)
+            if within(first):
+                products("alpha", first)
+            if within(early):
+                products("sigma", early)
+            if within(third):
+                products("mu", third)
 
         total = late.tile([P, 2, D], F32)
         nc.scalar.activation(out=total[:], in_=sums[:], func=FUNC.Ln)

@@ -362,18 +362,22 @@ def tile_rnadeoutputlayer_e_kernel(
             if within(third):
                 products("mu", third)
 
-        total = late.tile([P, 2, D], F32)
-        nc.scalar.activation(out=total[:], in_=sums[:], func=FUNC.Ln)
-        lse = late.tile([P, 2, D], F32)
-        nc.vector.tensor_tensor(out=lse[:], in0=total[:], in1=least[:], op=ALU.subtract)
-        per_d = late.tile([P, D], F32)
-        nc.vector.tensor_tensor(out=per_d[:], in0=lse[:, 1, :], in1=lse[:, 0, :], op=ALU.subtract)
-        result = late.tile([P, 1], F32)
-        nc.vector.tensor_reduce(out=result[:], in_=per_d[:], axis=AXIS.X, op=ALU.add)
-
+        gap = late.tile([P, D], F32)
+        nc.vector.tensor_tensor(out=gap[:], in0=least[:, 0, :], in1=least[:, 1, :], op=ALU.subtract)
+        shift = late.tile([P, 1], F32)
+        nc.vector.tensor_reduce(out=shift[:], in_=gap[:], axis=AXIS.X, op=ALU.add)
+        nc.vector.reciprocal(out=sums[:, 0, :], in_=sums[:, 0, :])
         as_rows = psum_tr.tile([P, P], F32, tag="tr")
-        nc.tensor.transpose(
-            out=as_rows[:], in_=result[:, 0:1].to_broadcast([P, P]), identity=ident_f32[:]
+        nc.tensor.matmul(
+            out=as_rows[:], lhsT=shift[:, 0:1].to_broadcast([P, P]), rhs=ident_f32[:],
+            is_transpose=True, start=True, stop=False,
+        )
+        logs = late.tile([P, 2, D], F32)
+        log_sum = late.tile([P, 1], F32)
+        nc.scalar.activation(out=logs[:], in_=sums[:], func=FUNC.Ln, accum_out=log_sum[:])
+        nc.tensor.matmul(
+            out=as_rows[:], lhsT=log_sum[:, 0:1].to_broadcast([P, P]), rhs=ident_f32[:],
+            is_transpose=True, start=False, stop=True,
         )
         out_row = late.tile([P, P], F32)
         nc.vector.tensor_scalar_add(out=out_row[:], in0=as_rows[:], scalar1=-D * HALF_LOG_2PI)

from contextlib import ExitStack
import math

import concourse.mybir as mybir
from concourse.masks import make_identity

F32 = mybir.dt.float32
BF16 = mybir.dt.bfloat16
I32 = mybir.dt.int32
U8 = mybir.dt.uint8
FP8X4 = mybir.dt.float8_e4m3fn_x4
ALU = mybir.AluOpType
FUNC = mybir.ActivationFunctionType
AXIS = mybir.AxisListType

MANUAL = True

P = 128
B = 128
E = 128
H = 512
D = 64
PACK = 4
DB = 4
NB = D // DB
XB = 8
XRAW_BUFS = 8
EP = 16
NP = E // EP
WRAW_BUFS = 6
AHEAD = 4
HALF_LOG_2PI = 0.5 * math.log(2.0 * math.pi)

FLOPS = 2 * B * E * H * D * 3


def tile_rnadeoutputlayer_e_kernel(
    tc,
    x,
    input_var,
    V_alpha_words,
    V_alpha_scales,
    V_mu_words,
    V_mu_scales,
    V_sigma_words,
    V_sigma_scales,
    b_alpha,
    b_mu,
    b_sigma,
    out,
):
    nc = tc.nc
    words_of = {"alpha": V_alpha_words, "sigma": V_sigma_words, "mu": V_mu_words}
    scales_of = {"alpha": V_alpha_scales, "sigma": V_sigma_scales, "mu": V_mu_scales}
    bias_of = {"alpha": b_alpha, "sigma": b_sigma, "mu": b_mu}
    kinds = ("alpha", "sigma", "mu")

    with ExitStack() as ctx:
        if MANUAL:
            ctx.enter_context(tc.manual_schedule())
        keep = ctx.enter_context(tc.tile_pool(name="keep", bufs=1))
        wraw_pool = ctx.enter_context(tc.tile_pool(name="wraw", bufs=WRAW_BUFS))
        wm_first = ctx.enter_context(tc.tile_pool(name="wm_first", bufs=1))

        y_bf = keep.tile([P, D], BF16)
        nc.scalar.dma_start(out=y_bf[:], in_=input_var)
        bias_sb = {}
        for kind in kinds:
            bias_tile = keep.tile([P, D], BF16, name="bias_%s" % kind)
            nc.scalar.dma_start(out=bias_tile[:], in_=bias_of[kind])
            bias_sb[kind] = bias_tile
        ident_bf = keep.tile([P, P], BF16)
        make_identity(nc, ident_bf[:])
        ident_f32 = keep.tile([P, P], F32)
        make_identity(nc, ident_f32[:])

        xq = keep.tile([P, D, B], I32, align_bytes=64)
        xq_scales = keep.tile([P, D, B], U8, align_bytes=64)
        planes = keep.tile([P, D, E], U8, align_bytes=64)
        y_table = keep.tile([P, D, B], BF16)
        neg_ba = keep.tile([P, D], F32)
        neg_bs = keep.tile([P, D], F32)
        bm32 = keep.tile([P, D], F32)
        hi = keep.tile([P, D], F32)
        lo = keep.tile([P, D], F32)
        least = keep.tile([P, 2, D], F32)
        sums = keep.tile([P, 2, D], F32)

        wm = {}
        pieces = [(kind, j) for kind in kinds for j in range(NP)]
        wraw = {}

        def load_piece(index):
            kind, j = pieces[index]
            raw = wraw_pool.tile([P, EP, D], I32, tag="wraw", align_bytes=1024)
            wraw[index] = raw
            nc.sync.dma_start(
                out=raw[:],
                in_=words_of[kind][EP * j : EP * (j + 1)]
                .rearrange("e p d t -> e p (d t)")
                .bitcast(I32)
                .rearrange("e p d -> p e d"),
            )

        def regroup_piece(index):
            kind, j = pieces[index]
            nc.vector.tensor_copy(
                out=wm[kind][:, :, EP * j : EP * (j + 1)].rearrange("p (g i) e -> p g e i", i=4),
                in_=wraw[index][:].rearrange("p e (g i) -> p g e i", i=4),
            )
            if index + WRAW_BUFS < len(pieces):
                load_piece(index + WRAW_BUFS)

        wm_alpha = wm_first.tile([P, D, E], I32, tag="wm", align_bytes=64)
        wm["alpha"] = wm_alpha

        with tc.tile_pool(name="xstage", bufs=1) as xstage, tc.psum_pool(name="psum_x", bufs=2) as psum_x:
            raw_planes = xstage.tile([P, E, D], U8, align_bytes=1024)
            nc.vector.memset(raw_planes[:].rearrange("p e d -> p (e d)").bitcast(I32), 0)
            grouped = xstage.tile([P, D, B, PACK], BF16, align_bytes=64)
            xraw = {}

            def load_x(i):
                raw = xstage.tile([P, XB, PACK * D], BF16, tag="xraw", bufs=XRAW_BUFS, align_bytes=1024)
                xraw[i] = raw
                nc.sync.dma_start(
                    out=raw[:],
                    in_=x[XB * i : XB * (i + 1), :, :].rearrange("b (p t) d -> p b (t d)", t=PACK),
                )

            staged_planes = xstage.tile([P, E, D], U8, align_bytes=1024)
            for ki in range(len(kinds)):
                nc.sync.dma_start(
                    out=staged_planes[32 * ki : 32 * ki + 16, :, :].bitcast(I32),
                    in_=scales_of[kinds[ki]].bitcast(I32).rearrange("e q g -> q e g"),
                )

            scale_moves = [(ki, quad) for ki in range(len(kinds)) for quad in range(4)]

            def move_scale_rows(ki, quad):
                nc.sync.dma_start(
                    out=raw_planes[32 * quad + 4 * ki : 32 * quad + 4 * ki + 4, :, :].bitcast(I32),
                    in_=staged_planes[32 * ki + 4 * quad : 32 * ki + 4 * quad + 4, :, :].bitcast(I32),
                )

            def regroup_planes(a):
                cols = slice(16 * a, 16 * (a + 1))
                nc.vector.tensor_copy(
                    out=planes[:, cols, :].rearrange("p (g i) e -> p g e i", i=4),
                    in_=raw_planes[:, :, cols].rearrange("p e (g i) -> p g e i", i=4),
                )

            for i in range(XRAW_BUFS):
                load_x(i)
            for i in range(B // XB):
                dst = grouped[:, :, XB * i : XB * (i + 1), :].rearrange("p (c i) b t -> p c (b t) i", i=4)
                src = xraw[i][:].rearrange("p b (t c i) -> p c (b t) i", t=PACK, i=4)
                if i % 3 == 1:
                    nc.scalar.copy(out=dst, in_=src)
                else:
                    nc.vector.tensor_copy(out=dst, in_=src)
                for ki, quad in scale_moves[6 * i : 6 * (i + 1)]:
                    move_scale_rows(ki, quad)
                if i + XRAW_BUFS < B // XB:
                    load_x(i + XRAW_BUFS)
                if i == 2:
                    nc.vector.tensor_tensor(out=neg_ba[:], in0=bias_sb["sigma"][:], in1=bias_sb["alpha"][:], op=ALU.subtract)
                    nc.vector.tensor_scalar(out=neg_bs[:], in0=bias_sb["sigma"][:], scalar1=-1.0, scalar2=0.0, op0=ALU.mult, op1=ALU.add)
                    nc.vector.tensor_scalar(out=hi[:], in0=bias_sb["sigma"][:], scalar1=-1.0, scalar2=20.0, op0=ALU.mult, op1=ALU.add)
                    nc.vector.tensor_scalar(out=lo[:], in0=bias_sb["sigma"][:], scalar1=-1.0, scalar2=-20.0, op0=ALU.mult, op1=ALU.add)
                    nc.vector.tensor_copy(out=bm32[:], in_=bias_sb["mu"][:])
                if i >= 12:
                    regroup_planes(i - 12)
                spread = psum_x.tile([P, DB, B], BF16, tag="spread")
                for k in range(DB):
                    d = DB * i + k
                    nc.tensor.transpose(
                        out=spread[:, k, :],
                        in_=y_bf[:, d : d + 1].to_broadcast([P, P]),
                        identity=ident_bf[:],
                    )
                nc.scalar.copy(out=y_table[:, DB * i : DB * (i + 1), :], in_=spread[:])

            for index in range(WRAW_BUFS):
                load_piece(index)

            for g8 in range(D // 8):
                d_cols = slice(8 * g8, 8 * g8 + 8)
                nc.vector.quantize_mx(
                    out=xq[:, d_cols, :].rearrange("p d b -> p (d b)").bitcast(FP8X4),
                    scales=xq_scales[:, d_cols, :].rearrange("p d b -> p (d b)"),
                    in_=grouped[:, d_cols, :, :].rearrange("p d b t -> p (d b t)"),
                )
                if g8 % 2 == 1:
                    regroup_piece(g8 // 2)
            for index in range(4, NP):
                regroup_piece(index)

        late = ctx.enter_context(tc.tile_pool(name="late", bufs=1, reuse_waits="tile"))
        psum_mx = ctx.enter_context(tc.psum_pool(name="psum_mx", bufs=4, reuse_waits="tile"))
        psum_tr = ctx.enter_context(tc.psum_pool(name="psum_tr", bufs=4, reuse_waits="tile"))

        neg_a = late.tile([P, D, B], F32)
        wm_sigma = late.tile([P, D, E], I32, align_bytes=64)
        wm["sigma"] = wm_sigma

        banks = {}
        turned = {}
        clipped = {}
        inv_sigma = {}
        dev = {}

        def products(kind, n):
            bank = psum_mx.tile([P, DB, B], F32, tag="mx")
            banks[(kind, n)] = bank
            first_row = 4 * kinds.index(kind)
            for k in range(DB):
                d = DB * n + k
                nc.tensor.matmul_mx(
                    out=bank[:, k, :],
                    lhsT=wm[kind][:, d, :].bitcast(FP8X4),
                    lhsT_scale=planes[first_row:P, d, :],
                    rhs=xq[:, d, :].bitcast(FP8X4),
                    rhs_scale=xq_scales[:, d, :],
                    start=True,
                    stop=True,
                )

        def take_alpha(n):
            for k in range(DB):
                d = DB * n + k
                nc.scalar.activation(
                    out=neg_a[:, d, :], in_=banks[("alpha", n)][:, k, :], func=FUNC.Identity,
                    bias=neg_ba[:, d : d + 1], scale=-1.0,
                )

        def turn_alpha(n):
            bank = psum_tr.tile([P, DB, E], F32, tag="tr")
            turned[(0, n)] = bank
            for k in range(DB):
                d = DB * n + k
                nc.tensor.matmul(
                    out=bank[:, k, :], lhsT=neg_bs[:, d : d + 1].to_broadcast([P, P]), rhs=ident_f32[:],
                    is_transpose=True, start=(k == 0), stop=False,
                )
            for k in range(DB):
                nc.tensor.matmul(
                    out=bank[:, k, :], lhsT=neg_a[:, DB * n + k, :], rhs=ident_f32[:],
                    is_transpose=True, start=False, stop=(k == DB - 1),
                )

        def least_of(which, n):
            nc.vector.tensor_reduce(
                out=least[:, which, DB * n : DB * (n + 1)], in_=turned[(which, n)][:], axis=AXIS.X, op=ALU.min
            )

        def exponentials(which, n):
            for k in range(DB):
                d = DB * n + k
                exp_out = late.tile([P, E], BF16, tag="exp_out", bufs=2)
                nc.scalar.activation(
                    out=exp_out[:], in_=turned[(which, n)][:, k, :], func=FUNC.Exp,
                    bias=least[:, which, d : d + 1], scale=-1.0, accum_out=sums[:, which, d : d + 1],
                )

        def take_sigma(n):
            sc = late.tile([P, DB, B], F32, tag="clipped", bufs=6 + AHEAD)
            clipped[n] = sc
            for k in range(DB):
                d = DB * n + k
                nc.vector.tensor_scalar(
                    out=sc[:, k, :], in0=banks[("sigma", n)][:, k, :],
                    scalar1=hi[:, d : d + 1], scalar2=lo[:, d : d + 1], op0=ALU.min, op1=ALU.max,
                )

        def exp_sigma(n):
            inv = late.tile([P, DB, B], F32, tag="inv", bufs=3 + AHEAD)
            inv_sigma[n] = inv
            for k in range(DB):
                d = DB * n + k
                nc.scalar.activation(
                    out=inv[:, k, :], in_=clipped[n][:, k, :], func=FUNC.Exp,
                    bias=neg_bs[:, d : d + 1], scale=-1.0,
                )

        def take_mu(n):
            m = late.tile([P, DB, B], F32, tag="dev", bufs=6)
            dev[n] = m
            for k in range(DB):
                d = DB * n + k
                nc.vector.scalar_tensor_tensor(
                    out=m[:, k, :], in0=banks[("mu", n)][:, k, :], scalar=bm32[:, d : d + 1],
                    in1=y_table[:, d, :], op0=ALU.add, op1=ALU.subtract,
                )

        def scale_dev(n):
            nc.gpsimd.tensor_tensor(out=dev[n][:], in0=dev[n][:], in1=inv_sigma[n][:], op=ALU.mult)

        def half_square(n):
            nc.scalar.activation(out=dev[n][:], in_=dev[n][:], func=FUNC.Square, scale=math.sqrt(0.5))

        def turn_density(n):
            bank = psum_tr.tile([P, DB, E], F32, tag="tr")
            turned[(1, n)] = bank
            for k in range(DB):
                nc.tensor.matmul(
                    out=bank[:, k, :], lhsT=neg_a[:, DB * n + k, :], rhs=ident_f32[:],
                    is_transpose=True, start=(k == 0), stop=False,
                )
            for k in range(DB):
                nc.tensor.matmul(
                    out=bank[:, k, :], lhsT=clipped[n][:, k, :], rhs=ident_f32[:],
                    is_transpose=True, start=False, stop=False,
                )
            for k in range(DB):
                nc.tensor.matmul(
                    out=bank[:, k, :], lhsT=dev[n][:, k, :], rhs=ident_f32[:],
                    is_transpose=True, start=False, stop=(k == DB - 1),
                )

        def within(n):
            return 0 <= n < NB

        for t in range(3 * NB + 8):
            first = t
            second = t - NB
            third = t - 2 * NB
            early = third + AHEAD
            if within(third - 7):
                exponentials(1, third - 7)
            if within(third - 6):
                least_of(1, third - 6)
            if within(third - 5):
                turn_density(third - 5)
            if within(third - 4):
                half_square(third - 4)
            if within(third - 3):
                scale_dev(third - 3)
            if within(early - 2):
                exp_sigma(early - 2)
            if within(second - 2):
                exponentials(0, second - 2)
            if within(second - 1):
                least_of(0, second - 1)
            if within(early - 1):
                take_sigma(early - 1)
            if within(third - 1):
                take_mu(third - 1)
            if within(first - 1):
                take_alpha(first - 1)
            if t < 2 * NB and t % 2 == 0:
                if t == NB:
                    wm_mu = wm_first.tile([P, D, E], I32, tag="wm", align_bytes=64)
                    wm["mu"] = wm_mu
                regroup_piece(NP + t // 2)
            if within(second):
                turn_alpha(second)
            if within(first):
                products("alpha", first)
            if within(early):
                products("sigma", early)
            if within(third):
                products("mu", third)

        gap = late.tile([P, D], F32)
        nc.vector.tensor_tensor(out=gap[:], in0=least[:, 0, :], in1=least[:, 1, :], op=ALU.subtract)
        shift = late.tile([P, 1], F32)
        nc.vector.tensor_reduce(out=shift[:], in_=gap[:], axis=AXIS.X, op=ALU.add)
        nc.vector.reciprocal(out=sums[:, 0, :], in_=sums[:, 0, :])
        as_rows = psum_tr.tile([P, P], F32, tag="tr")
        nc.tensor.matmul(
            out=as_rows[:], lhsT=shift[:, 0:1].to_broadcast([P, P]), rhs=ident_f32[:],
            is_transpose=True, start=True, stop=False,
        )
        logs = late.tile([P, 2, D], F32)
        log_sum = late.tile([P, 1], F32)
        nc.scalar.activation(out=logs[:], in_=sums[:], func=FUNC.Ln, accum_out=log_sum[:])
        nc.tensor.matmul(
            out=as_rows[:], lhsT=log_sum[:, 0:1].to_broadcast([P, P]), rhs=ident_f32[:],
            is_transpose=True, start=False, stop=True,
        )
        out_row = late.tile([P, P], F32)
        nc.vector.tensor_scalar_add(out=out_row[:], in0=as_rows[:], scalar1=-D * HALF_LOG_2PI)
        nc.sync.dma_start(out=out.rearrange("(o b) -> o b", o=1), in_=out_row[0:1, :])
